import numpy as np
import ml_dtypes


def mxq(x, axis, fmt="e4m3"):
    dtype, down = {"e4m3": (ml_dtypes.float8_e4m3fn, 7), "e5m2": (ml_dtypes.float8_e5m2, 14)}[fmt]
    v = np.moveaxis(np.asarray(x, np.float32).astype(ml_dtypes.bfloat16).astype(np.float64), axis, -1)
    blocks = v.reshape(v.shape[:-1] + (-1, 32))
    amax = np.abs(blocks).max(-1, keepdims=True)
    byte = np.maximum(np.where(amax > 0, np.frexp(amax)[1] - 1 + 127, 0) - down, 1)
    scale = np.exp2(byte - 127.0)
    codes = (blocks / scale).astype(np.float32).astype(dtype).astype(np.float64)
    return np.moveaxis((codes * scale).reshape(v.shape), -1, axis)


BF16 = ml_dtypes.bfloat16


def bf(x):
    return np.asarray(x, np.float32).astype(BF16)


def f64(x):
    return np.asarray(x).astype(np.float64)


B, S, D, DV = 16, 512, 128, 512
EPS = 1e-6
C0 = 0.01
G = 4


def points(ctr, rad):
    g = np.random.randint(G, size=(B, S))
    b = np.arange(B)[:, None]
    sig = np.exp2(-np.random.uniform(1.0, 5.0, (B, S, 1)))
    p = ctr[b, g] + sig * np.random.standard_normal((B, S, D)) / np.sqrt(D)
    return p / np.linalg.norm(p, axis=-1, keepdims=True) * rad[b, g][:, :, None]


def setup_inputs():
    c = bf(C0 * (1.0 + 0.1 * np.random.standard_normal(1)))
    ctr = np.random.standard_normal((B, G, D))
    ctr = ctr / np.linalg.norm(ctr, axis=-1, keepdims=True)
    rho = np.linspace(0.7, 1.1, G) + np.random.uniform(-0.03, 0.03, (B, G))
    rad = np.sqrt(rho / f64(c)[0])
    return {"query": bf(points(ctr, rad)), "keys": bf(points(ctr, rad)),
            "values": bf(np.random.standard_normal((B, S, DV)) * 0.25 * np.sqrt(S)), "c": c}


def reference(query, keys, values, c):
    query, keys, values, c = f64(query), f64(keys), f64(values), f64(c)
    scale = np.sqrt(D)
    q2 = np.sum(query * query, axis=-1)
    k2 = np.sum(keys * keys, axis=-1)
    cross = query @ keys.transpose(0, 2, 1)
    nd2 = np.maximum(q2[:, :, None] + k2[:, None, :] - 2.0 * cross, 0.0)
    denom = np.maximum((1.0 - c * q2) * (1.0 - c * k2), EPS)
    arg = np.maximum(1.0 + 2.0 * c * nd2 / denom[:, :, None], 1.0 + EPS)
    dist = np.arccosh(arg)
    lg = -dist / scale
    e = np.exp(lg - lg.max(-1, keepdims=True))
    return (mxq(e, 2, "e4m3") @ mxq(values, 1, "e4m3")) / e.sum(-1, keepdims=True)

@@ -1,0 +1,429 @@
+from contextlib import ExitStack
+import math
+
+import concourse.mybir as mybir
+from concourse.masks import make_identity
+
+F32 = mybir.dt.float32
+BF16 = mybir.dt.bfloat16
+U32 = mybir.dt.uint32
+U8 = mybir.dt.uint8
+FP8X4 = mybir.dt.float8_e4m3fn_x4
+AF = mybir.ActivationFunctionType
+ALU = mybir.AluOpType
+
+NB, S, D, DV = 16, 512, 128, 512
+P = 128
+NT = S // P
+EPS = 1e-6
+KAPPA = 2.0 ** -21
+INV_SCALE2 = 2.0 / math.sqrt(D)
+W1 = S + 1
+WP = S + 8
+FLOPS = 2 * NB * S * S * (D + DV)
+
+GB = 4
+NG = NB // GB
+CHUNKS = ((0,), (1,), (2, 3), (4, 5, 6, 7), (8, 9, 10, 11), (12, 13, 14, 15))
+NV = 4
+NVC = 6
+NP_, NE_, NO_ = 3, 2, 2
+G2N, B0, B1, HI, NK2H = 4, 5, 6, 7, 8
+
+
+def tile_hyperbolicattention_t_kernel(tc, query, keys, values, c, out):
+    nc = tc.nc
+    with ExitStack() as ctx:
+        ctx.enter_context(tc.manual_schedule())
+        const = ctx.enter_context(tc.tile_pool(name="const", bufs=1))
+        qktp = ctx.enter_context(tc.tile_pool(name="qktp", bufs=2))
+        xp = ctx.enter_context(tc.tile_pool(name="xp", bufs=GB))
+        rp = ctx.enter_context(tc.tile_pool(name="rp", bufs=GB))
+        smallp = ctx.enter_context(tc.tile_pool(name="smallp", bufs=2 * GB))
+        ep = ctx.enter_context(tc.tile_pool(name="ep", bufs=GB))
+        grpp = ctx.enter_context(tc.tile_pool(name="grpp", bufs=2))
+        ecp = ctx.enter_context(tc.tile_pool(name="ecp", bufs=2))
+        vnp = ctx.enter_context(tc.tile_pool(name="vnp", bufs=NV))
+        vgp = ctx.enter_context(tc.tile_pool(name="vgp", bufs=2))
+        vcp = ctx.enter_context(tc.tile_pool(name="vcp", bufs=NVC))
+        ostp = ctx.enter_context(tc.tile_pool(name="ostp", bufs=2))
+        ps_p = ctx.enter_context(tc.psum_pool(name="ps_p", bufs=NP_))
+        ps_q = ctx.enter_context(tc.psum_pool(name="ps_q", bufs=1))
+        ps_e = ctx.enter_context(tc.psum_pool(name="ps_e", bufs=NE_))
+        ps_o = ctx.enter_context(tc.psum_pool(name="ps_o", bufs=NO_))
+
+        chunk_of = {}
+        for ci, ch in enumerate(CHUNKS):
+            for b in ch:
+                chunk_of[b] = ci
+
+        def col(b, t):
+            return (b - CHUNKS[chunk_of[b]][0]) * NT + t
+
+        c_bf = const.tile([P, 1], BF16, name="c_bf")
+        nc.sync.dma_start(out=c_bf[:], in_=c.partition_broadcast(P))
+        ident_bf = const.tile([P, P], BF16, name="ident_bf")
+        make_identity(nc, ident_bf[:])
+        ident_f = const.tile([P, P], F32, name="ident_f")
+        make_identity(nc, ident_f[:])
+        one = const.tile([P, 1], F32, name="one")
+        nc.vector.memset(one[:], 1.0)
+        warm = const.tile([P, 1], F32, name="warm")
+        nc.scalar.activation(out=warm[:], in_=one[:], func=AF.Sqrt)
+        junk = const.tile([P, D], BF16, name="junk")
+        cc = const.tile([P, 8], F32, name="cc")
+        cf, negc, neg2c, rc, e4c = (cc[:, i : i + 1] for i in range(5))
+        nc.vector.tensor_copy(out=cf, in_=c_bf[:])
+        nc.vector.tensor_scalar_mul(out=negc, in0=cf, scalar1=-1.0)
+        nc.vector.tensor_scalar_mul(out=neg2c, in0=cf, scalar1=-2.0)
+        nc.vector.reciprocal(out=rc, in_=cf)
+        nc.vector.tensor_scalar_mul(out=e4c, in0=rc, scalar1=EPS / 4.0)
+
+        qn, kn, sq, cs, vn = {}, {}, {}, {}, {}
+        qkps, qkT, X, R, EB, RS, RI, E, ET, GRP, EC, ES, VG, VC, VS, PS, O, OST = ({} for i in range(18))
+
+        def load_qk(ci):
+            ch = CHUNKS[ci]
+            rows = slice(ch[0], ch[-1] + 1)
+            qn[ci] = const.tile([P, len(ch), S], BF16, name="qn%d" % ci)
+            kn[ci] = const.tile([P, len(ch), S], BF16, name="kn%d" % ci)
+            nc.sync.dma_start(out=qn[ci][:], in_=query[rows].rearrange("b (p t) d -> p b (t d)", t=NT))
+            nc.sync.dma_start(out=kn[ci][:], in_=keys[rows].rearrange("b (p t) d -> p b (t d)", t=NT))
+            sq[ci] = const.tile([P, 2, NT * len(ch)], F32, name="sq%d" % ci)
+
+        def rows_of(src, b, t):
+            ci = chunk_of[b]
+            return src[ci][:, b - CHUNKS[ci][0], t * D : (t + 1) * D]
+
+        def load_values(b):
+            vn[b] = vnp.tile([P, NT, DV], BF16, name="vn")
+            nc.sync.dma_start(out=vn[b][:], in_=values[b].rearrange("(p t) v -> p t v", t=NT))
+
+        def squares(b):
+            for which, src in ((0, qn), (1, kn)):
+                for t in range(NT):
+                    nc.scalar.activation(
+                        out=junk[:], in_=rows_of(src, b, t), func=AF.Square,
+                        accum_out=sq[chunk_of[b]][:, which, col(b, t) : col(b, t) + 1],
+                    )
+
+        def constants(ci):
+            n = NT * len(CHUNKS[ci])
+            t_ = const.tile([P, 9, n], F32, name="cs%d" % ci)
+            cs[ci] = t_
+            q2, k2 = sq[ci][:, 0, :], sq[ci][:, 1, :]
+            nc.vector.tensor_scalar(out=t_[:, 0:2, :], in0=sq[ci][:], scalar1=negc, scalar2=1.0, op0=ALU.mult, op1=ALU.add)
+            den = t_[:, 2, :]
+            nc.vector.tensor_tensor(out=den, in0=t_[:, 0, :], in1=t_[:, 1, :], op=ALU.mult)
+            nc.vector.tensor_scalar_max(out=den, in0=den, scalar1=EPS)
+            nc.vector.reciprocal(out=t_[:, 3, :], in_=den)
+            nc.vector.tensor_scalar(out=t_[:, G2N, :], in0=t_[:, 3, :], scalar1=neg2c, scalar2=None, op0=ALU.mult)
+            nc.vector.tensor_scalar_mul(out=t_[:, NK2H, :], in0=k2, scalar1=-0.5)
+            nc.vector.tensor_scalar(out=t_[:, 0, :], in0=den, scalar1=e4c, scalar2=None, op0=ALU.mult)
+            nc.vector.scalar_tensor_tensor(out=t_[:, HI, :], in0=q2, scalar=(1.0 - KAPPA) / 2.0, in1=t_[:, 0, :], op0=ALU.mult, op1=ALU.subtract)
+            nc.vector.scalar_tensor_tensor(out=t_[:, B0, :], in0=t_[:, G2N, :], scalar=-0.5, in1=q2, op0=ALU.mult, op1=ALU.mult)
+            nc.vector.tensor_scalar_add(out=t_[:, B1, :], in0=t_[:, B0, :], scalar1=1.0)
+
+        def cst(b, t, row):
+            return cs[chunk_of[b]][:, row, col(b, t) : col(b, t) + 1]
+
+        def transpose_qk(b):
+            qkps[b] = ps_q.tile([P, 2 * S], BF16, name="qk_ps")
+            for w, src in ((0, qn), (1, kn)):
+                for t in range(NT):
+                    nc.tensor.transpose(qkps[b][:, w * S + t * P : w * S + (t + 1) * P], rows_of(src, b, t), ident_bf[:])
+
+        def copy_qk(b):
+            qkT[b] = qktp.tile([P, 2 * S], BF16, name="qkT")
+            nc.vector.tensor_copy(out=qkT[b][:], in_=qkps[b][:])
+
+        def cross(b, t):
+            ps = ps_p.tile([P, S], F32, name="P")
+            PS[b, t] = ps
+            nc.tensor.matmul(out=ps[:], lhsT=qkT[b][:, t * P : (t + 1) * P], rhs=qkT[b][:, S : 2 * S], start=True, stop=False)
+            for tj in range(NT):
+                nc.tensor.matmul(
+                    out=ps[:, tj * P : (tj + 1) * P], lhsT=cst(b, tj, NK2H).to_broadcast([P, P]), rhs=ident_f[:],
+                    is_transpose=True, start=False, stop=(tj == NT - 1),
+                )
+
+        def clamp(b, t):
+            if t == 0:
+                X[b] = xp.tile([P, NT, WP], F32, name="X")
+            nc.vector.tensor_scalar(
+                out=X[b][:, t, 0:S], in0=PS[b, t][:], scalar1=cst(b, t, HI), scalar2=None,
+                op0=ALU.min, op1=ALU.max, accum_out=X[b][:, t, S:W1],
+            )
+
+        def roots(b):
+            R[b] = rp.tile([P, NT, WP], F32, name="R")
+            for t in range(NT):
+                nc.scalar.activation(out=R[b][:, t, 0:W1], in_=X[b][:, t, 0:W1], func=AF.Sqrt, bias=cst(b, t, B1), scale=cst(b, t, G2N))
+                nc.scalar.activation(out=X[b][:, t, 0:W1], in_=X[b][:, t, 0:W1], func=AF.Sqrt, bias=cst(b, t, B0), scale=cst(b, t, G2N))
+
+        def add_roots(b):
+            nc.vector.tensor_tensor(out=R[b][:, :, 0:W1], in0=R[b][:, :, 0:W1], in1=X[b][:, :, 0:W1], op=ALU.add)
+
+        def logs(b):
+            nc.scalar.activation(out=R[b][:, :, 0:W1], in_=R[b][:, :, 0:W1], func=AF.Ln)
+            EB[b] = smallp.tile([P, NT], F32, name="eb")
+            nc.scalar.mul(out=EB[b][:].unsqueeze(2), in_=R[b][:, :, S:W1], mul=INV_SCALE2)
+
+        def exps(b):
+            E[b] = ep.tile([P, NT, S], BF16, name="e")
+            RS[b] = smallp.tile([P, NT], F32, name="rs")
+            for t in range(NT):
+                nc.scalar.activation(
+                    out=E[b][:, t, :], in_=R[b][:, t, 0:S], func=AF.Exp,
+                    bias=EB[b][:, t : t + 1], scale=-INV_SCALE2, accum_out=RS[b][:, t : t + 1],
+                )
+
+        def recip(b):
+            RI[b] = smallp.tile([P, NT], F32, name="ri")
+            nc.vector.reciprocal(out=RI[b][:], in_=RS[b][:])
+
+        def transpose_e(b, h):
+            ET[b, h] = ps_e.tile([P, 2, NT, P], BF16, name="eT")
+            for a in range(2):
+                for tj in range(NT):
+                    nc.tensor.transpose(ET[b, h][:, a, tj, :], E[b][:, 2 * h + a, tj * P : (tj + 1) * P], ident_bf[:])
+
+        def copy_e(b, h, eng):
+            if h == 0:
+                GRP[b] = grpp.tile([P, S, NT], BF16, name="grp", align_bytes=64)
+            dst = GRP[b][:, h * 2 * P : (h + 1) * 2 * P, :].rearrange("p (a i) t -> p a i t", a=2)
+            src = ET[b, h][:].rearrange("p a t i -> p a i t")
+            if eng == "act":
+                nc.scalar.copy(out=dst, in_=src)
+            else:
+                nc.vector.tensor_copy(out=dst, in_=src)
+
+        def quantise_e(b):
+            EC[b] = ecp.tile([P, S], U32, name="ec", align_bytes=64)
+            ES[b] = ecp.tile([P, S], U8, name="es", align_bytes=64)
+            nc.vector.quantize_mx(out=EC[b][:].bitcast(FP8X4), scales=ES[b][:], in_=GRP[b][:].rearrange("p i t -> p (i t)"))
+
+        def regroup_v(b):
+            VG[b] = vgp.tile([P, DV, NT], BF16, name="vg", align_bytes=64)
+            nc.vector.tensor_copy(
+                out=VG[b][:].rearrange("p (c i) t -> p c t i", i=4),
+                in_=vn[b][:].rearrange("p t (c i) -> p c t i", i=4),
+            )
+
+        def quantise_v(b):
+            VC[b] = vcp.tile([P, DV], U32, name="vc", align_bytes=64)
+            VS[b] = vcp.tile([P, DV], U8, name="vs", align_bytes=64)
+            nc.vector.quantize_mx(out=VC[b][:].bitcast(FP8X4), scales=VS[b][:], in_=VG[b][:].rearrange("p v t -> p (v t)"))
+
+        def mx(b, t):
+            O[b, t] = ps_o.tile([P, DV], F32, name="O")
+            cols = slice(t * P, (t + 1) * P)
+            nc.tensor.matmul_mx(
+                out=O[b, t][:], lhsT=EC[b][:, cols].bitcast(FP8X4), lhsT_scale=ES[b][:, cols],
+                rhs=VC[b][:].bitcast(FP8X4), rhs_scale=VS[b][:], start=True, stop=True,
+            )
+
+        def scale_out(b, t, eng):
+            if t == 0:
+                OST[b] = ostp.tile([P, NT, DV], F32, name="ost")
+            if eng == "act":
+                nc.scalar.activation(out=OST[b][:, t, :], in_=O[b, t][:], func=AF.Copy, scale=RI[b][:, t : t + 1])
+            else:
+                nc.vector.tensor_scalar_mul(out=OST[b][:, t, :], in0=O[b, t][:], scalar1=RI[b][:, t : t + 1])
+
+        def store(b):
+            nc.sync.dma_start(out=out[b].rearrange("(p t) v -> p t v", t=NT), in_=OST[b][:])
+
+        order = {"act": [], "dve": [], "pe": [], "sp": []}
+        ring = {"P": [], "eT": [], "O": [], "qk": []}
+
+        def add(eng, key, needs, fn):
+            order[eng].append((key, [n for n in needs if n is not None], fn))
+
+        def back(name, key, depth):
+            lst = ring[name]
+            lst.append(key)
+            return lst[-1 - depth] if len(lst) > depth else None
+
+        def ok(kind, b, *rest):
+            return (kind, b) + rest if 0 <= b < NB else None
+
+        def t_sq(b):
+            add("act", ("sq", b), [("ldqk", chunk_of[b])], lambda: squares(b))
+
+        def t_roots(b):
+            add("act", ("roots", b), [("clamp", b, t) for t in range(NT)] + [ok("exps", b - GB)], lambda: roots(b))
+
+        def t_logs(b):
+            add("act", ("logs", b), [("add", b)], lambda: logs(b))
+
+        def t_exps(b):
+            add("act", ("exps", b), [("logs", b), ok("te", b - GB, 1)], lambda: exps(b))
+
+        def t_const(ci):
+            add("dve", ("const", ci), [("sq", b) for b in CHUNKS[ci]], lambda: constants(ci))
+
+        def t_prep_pe(b):
+            add("pe", ("tqk", b), [("ldqk", chunk_of[b]), back("qk", ("cqk", b), 1)], lambda: transpose_qk(b))
+
+        def t_cqk(b):
+            add("dve", ("cqk", b), [("tqk", b), ok("cross", b - 2, NT - 1)], lambda: copy_qk(b))
+
+        def t_cross(b):
+            for t in range(NT):
+                add("pe", ("cross", b, t), [("cqk", b), ("const", chunk_of[b]), back("P", ("clamp", b, t), NP_)], lambda t=t: cross(b, t))
+
+        def t_clamp(b):
+            for t in range(NT):
+                add("dve", ("clamp", b, t), [("cross", b, t), ok("add", b - GB)], lambda t=t: clamp(b, t))
+
+        def t_add(b):
+            add("dve", ("add", b), [("roots", b)], lambda: add_roots(b))
+
+        def t_te(b):
+            for h in range(2):
+                add("pe", ("te", b, h), [("exps", b), back("eT", ("ce", b, h), NE_)], lambda h=h: transpose_e(b, h))
+
+        def t_ce(b, h, eng="dve"):
+            add(eng, ("ce", b, h), [("te", b, h), ok("qe", b - 2)], lambda: copy_e(b, h, eng))
+
+        def t_qe(b):
+            add("dve", ("qe", b), [("ce", b, 0), ("ce", b, 1), ok("mx", b - 2, NT - 1)], lambda: quantise_e(b))
+
+        def t_vr(b):
+            add("dve", ("vr", b), [("ldv", b), ok("vq", b - 2)], lambda: regroup_v(b))
+
+        def t_vq(b):
+            add("dve", ("vq", b), [("vr", b), ok("mx", b - NVC, NT - 1)], lambda: quantise_v(b))
+
+        def t_mx(b):
+            for t in range(NT):
+                add("pe", ("mx", b, t), [("qe", b), ("vq", b), back("O", ("so", b, t), NO_)], lambda t=t: mx(b, t))
+
+        def t_recip(b):
+            add("dve", ("recip", b), [("exps", b)], lambda: recip(b))
+
+        def t_so(b, t, eng="dve"):
+            add(eng, ("so", b, t), [("mx", b, t), ("recip", b), ok("st", b - 2)], lambda: scale_out(b, t, eng))
+
+        def t_st(b):
+            add("sp", ("st", b), [("so", b, t) for t in range(NT)], lambda: store(b))
+
+        def t_ldv(b):
+            if b < NB:
+                add("sp", ("ldv", b), [ok("vr", b - NV)], lambda: load_values(b))
+
+        def t_ldqk(ci):
+            add("sp", ("ldqk", ci), [], lambda: load_qk(ci))
+
+        for ci in (0, 1, 2):
+            t_ldqk(ci)
+        t_ldv(0)
+        t_ldqk(3)
+        for b in (1, 2, 3):
+            t_ldv(b)
+        t_ldqk(4)
+        t_ldqk(5)
+
+        t_sq(0)
+        t_sq(1)
+        for g in range(NG):
+            for k in range(GB):
+                b = g * GB + k
+                t_roots(b)
+                if g == 0 and k < GB - 1:
+                    t_sq(2 * k + 2)
+                    t_sq(2 * k + 3)
+            for k in range(GB):
+                t_logs(g * GB + k)
+                if g + 2 < NG:
+                    t_sq((g + 2) * GB + k)
+            for k in range(GB):
+                t_exps(g * GB + k)
+
+        for b in range(GB):
+            t_prep_pe(b)
+            if b < 3:
+                t_const(b)
+            t_cqk(b)
+            t_cross(b)
+            t_clamp(b)
+            if b >= 1:
+                t_add(b - 1)
+        t_vr(0)
+        t_add(GB - 1)
+        t_vq(0)
+        t_ldv(NV)
+        t_const(3)
+        for k in range(1, GB):
+            nb = GB + k - 1
+            t_prep_pe(nb)
+            t_cqk(nb)
+            t_vr(k)
+            t_cross(nb)
+            t_vq(k)
+            t_ldv(NV + k)
+            t_clamp(nb)
+        t_const(4)
+
+        for g in range(1, NG):
+            for q in range(GB):
+                f = (g - 1) * GB + q
+                v = g * GB + q
+                r = g * GB + GB - 1 + q
+                if r < NB:
+                    t_prep_pe(r)
+                    t_cqk(r)
+                t_te(f)
+                t_ce(f, 0)
+                t_ce(f, 1)
+                if q == 1:
+                    t_add(g * GB + 1)
+                if q == 2:
+                    t_add(g * GB + 3)
+                t_vr(v)
+                t_qe(f)
+                t_vq(v)
+                t_ldv(v + NV)
+                if r < NB:
+                    t_cross(r)
+                    t_clamp(r)
+                t_mx(f)
+                t_recip(f)
+                for t in range(NT):
+                    t_so(f, t)
+                t_st(f)
+                if q == 0:
+                    t_add(g * GB)
+                if q == 1:
+                    t_add(g * GB + 2)
+            if g + 2 < NG:
+                t_const(g + 4)
+
+        for q in range(GB):
+            f = (NG - 1) * GB + q
+            shared = q >= 2
+            t_te(f)
+            t_ce(f, 0)
+            t_ce(f, 1, "act" if shared else "dve")
+            t_recip(f)
+            t_qe(f)
+            t_mx(f)
+            for t in range(NT):
+                t_so(f, t, "act" if (shared and t % 2 == 1) else "dve")
+            t_st(f)
+
+        done = set()
+        at = {e: 0 for e in order}
+        left = sum(len(v) for v in order.values())
+        while left:
+            moved = 0
+            for e in ("sp", "act", "pe", "dve"):
+                while at[e] < len(order[e]) and all(n in done for n in order[e][at[e]][1]):
+                    key, needs, fn = order[e][at[e]]
+                    fn()
+                    done.add(key)
+                    at[e] += 1
+                    moved += 1
+            assert moved, "the orders of the engines contradict each other"
+            left -= moved

@@ -25,9 +25,10 @@ FLOPS = 2 * NB * S * S * (D + DV)
 GB = 4
 NG = NB // GB
 CHUNKS = ((0,), (1,), (2, 3), (4, 5, 6, 7), (8, 9, 10, 11), (12, 13, 14, 15))
-NV = 4
-NVC = 6
-NP_, NE_, NO_ = 3, 2, 2
+NV = 3
+NVC = 3
+NP_, NE_, NO_ = 4, 2, 2
+ACT_SQUARES = GB
 G2N, B0, B1, HI, NK2H = 4, 5, 6, 7, 8
 
 
@@ -36,7 +37,7 @@ def tile_hyperbolicattention_t_kernel(tc, query, keys, values, c, out):
     with ExitStack() as ctx:
         ctx.enter_context(tc.manual_schedule())
         const = ctx.enter_context(tc.tile_pool(name="const", bufs=1))
-        qktp = ctx.enter_context(tc.tile_pool(name="qktp", bufs=2))
+        sqfp = ctx.enter_context(tc.tile_pool(name="sqfp", bufs=1))
         xp = ctx.enter_context(tc.tile_pool(name="xp", bufs=GB))
         rp = ctx.enter_context(tc.tile_pool(name="rp", bufs=GB))
         smallp = ctx.enter_context(tc.tile_pool(name="smallp", bufs=2 * GB))
@@ -44,11 +45,10 @@ def tile_hyperbolicattention_t_kernel(tc, query, keys, values, c, out):
         grpp = ctx.enter_context(tc.tile_pool(name="grpp", bufs=2))
         ecp = ctx.enter_context(tc.tile_pool(name="ecp", bufs=2))
         vnp = ctx.enter_context(tc.tile_pool(name="vnp", bufs=NV))
-        vgp = ctx.enter_context(tc.tile_pool(name="vgp", bufs=2))
+        vgp = ctx.enter_context(tc.tile_pool(name="vgp", bufs=GB))
         vcp = ctx.enter_context(tc.tile_pool(name="vcp", bufs=NVC))
         ostp = ctx.enter_context(tc.tile_pool(name="ostp", bufs=2))
         ps_p = ctx.enter_context(tc.psum_pool(name="ps_p", bufs=NP_))
-        ps_q = ctx.enter_context(tc.psum_pool(name="ps_q", bufs=1))
         ps_e = ctx.enter_context(tc.psum_pool(name="ps_e", bufs=NE_))
         ps_o = ctx.enter_context(tc.psum_pool(name="ps_o", bufs=NO_))
 
@@ -79,33 +79,45 @@ def tile_hyperbolicattention_t_kernel(tc, query, keys, values, c, out):
         nc.vector.reciprocal(out=rc, in_=cf)
         nc.vector.tensor_scalar_mul(out=e4c, in0=rc, scalar1=EPS / 4.0)
 
-        qn, kn, sq, cs, vn = {}, {}, {}, {}, {}
+        qk, sq, cs, vn, SQF = {}, {}, {}, {}, {}
         qkps, qkT, X, R, EB, RS, RI, E, ET, GRP, EC, ES, VG, VC, VS, PS, O, OST = ({} for i in range(18))
 
         def load_qk(ci):
             ch = CHUNKS[ci]
             rows = slice(ch[0], ch[-1] + 1)
-            qn[ci] = const.tile([P, len(ch), S], BF16, name="qn%d" % ci)
-            kn[ci] = const.tile([P, len(ch), S], BF16, name="kn%d" % ci)
-            nc.sync.dma_start(out=qn[ci][:], in_=query[rows].rearrange("b (p t) d -> p b (t d)", t=NT))
-            nc.sync.dma_start(out=kn[ci][:], in_=keys[rows].rearrange("b (p t) d -> p b (t d)", t=NT))
+            qk[ci] = const.tile([P, len(ch), 2, S], BF16, name="qk%d" % ci)
+            nc.sync.dma_start(out=qk[ci][:, :, 0, :], in_=query[rows].rearrange("b (p t) d -> p b (t d)", t=NT))
+            nc.sync.dma_start(out=qk[ci][:, :, 1, :], in_=keys[rows].rearrange("b (p t) d -> p b (t d)", t=NT))
             sq[ci] = const.tile([P, 2, NT * len(ch)], F32, name="sq%d" % ci)
 
-        def rows_of(src, b, t):
+        def rows_of(w, b, t):
             ci = chunk_of[b]
-            return src[ci][:, b - CHUNKS[ci][0], t * D : (t + 1) * D]
+            return qk[ci][:, b - CHUNKS[ci][0], w, t * D : (t + 1) * D]
 
         def load_values(b):
             vn[b] = vnp.tile([P, NT, DV], BF16, name="vn")
             nc.sync.dma_start(out=vn[b][:], in_=values[b].rearrange("(p t) v -> p t v", t=NT))
 
         def squares(b):
-            for which, src in ((0, qn), (1, kn)):
+            for w in range(2):
                 for t in range(NT):
                     nc.scalar.activation(
-                        out=junk[:], in_=rows_of(src, b, t), func=AF.Square,
-                        accum_out=sq[chunk_of[b]][:, which, col(b, t) : col(b, t) + 1],
+                        out=junk[:], in_=rows_of(w, b, t), func=AF.Square,
+                        accum_out=sq[chunk_of[b]][:, w, col(b, t) : col(b, t) + 1],
                     )
+
+        def square_mul(b):
+            ci = chunk_of[b]
+            SQF[b] = sqfp.tile([P, 2 * S], F32, name="sqf")
+            src = qk[ci][:, b - CHUNKS[ci][0], :, :].rearrange("p w s -> p (w s)")
+            nc.vector.tensor_tensor(out=SQF[b][:], in0=src, in1=src, op=ALU.mult)
+
+        def square_sum(b):
+            nc.vector.tensor_reduce(
+                out=sq[chunk_of[b]][:, :, col(b, 0) : col(b, 0) + NT],
+                in_=SQF[b][:].rearrange("p (w t d) -> p w t d", w=2, t=NT),
+                axis=mybir.AxisListType.X, op=ALU.add,
+            )
 
         def constants(ci):
             n = NT * len(CHUNKS[ci])
@@ -128,13 +140,13 @@ def tile_hyperbolicattention_t_kernel(tc, query, keys, values, c, out):
             return cs[chunk_of[b]][:, row, col(b, t) : col(b, t) + 1]
 
         def transpose_qk(b):
-            qkps[b] = ps_q.tile([P, 2 * S], BF16, name="qk_ps")
-            for w, src in ((0, qn), (1, kn)):
+            qkps[b] = ps_p.tile([P, 2 * S], BF16, name="P")
+            for w in range(2):
                 for t in range(NT):
-                    nc.tensor.transpose(qkps[b][:, w * S + t * P : w * S + (t + 1) * P], rows_of(src, b, t), ident_bf[:])
+                    nc.tensor.transpose(qkps[b][:, w * S + t * P : w * S + (t + 1) * P], rows_of(w, b, t), ident_bf[:])
 
         def copy_qk(b):
-            qkT[b] = qktp.tile([P, 2 * S], BF16, name="qkT")
+            qkT[b] = const.tile([P, 2 * S], BF16, name="qkT%d" % b)
             nc.vector.tensor_copy(out=qkT[b][:], in_=qkps[b][:])
 
         def cross(b, t):
@@ -162,7 +174,7 @@ def tile_hyperbolicattention_t_kernel(tc, query, keys, values, c, out):
                 nc.scalar.activation(out=X[b][:, t, 0:W1], in_=X[b][:, t, 0:W1], func=AF.Sqrt, bias=cst(b, t, B0), scale=cst(b, t, G2N))
 
         def add_roots(b):
-            nc.vector.tensor_tensor(out=R[b][:, :, 0:W1], in0=R[b][:, :, 0:W1], in1=X[b][:, :, 0:W1], op=ALU.add)
+            nc.gpsimd.tensor_tensor(out=R[b][:, :, 0:W1], in0=R[b][:, :, 0:W1], in1=X[b][:, :, 0:W1], op=ALU.add)
 
         def logs(b):
             nc.scalar.activation(out=R[b][:, :, 0:W1], in_=R[b][:, :, 0:W1], func=AF.Ln)
@@ -205,9 +217,8 @@ def tile_hyperbolicattention_t_kernel(tc, query, keys, values, c, out):
 
         def regroup_v(b):
             VG[b] = vgp.tile([P, DV, NT], BF16, name="vg", align_bytes=64)
-            nc.vector.tensor_copy(
-                out=VG[b][:].rearrange("p (c i) t -> p c t i", i=4),
-                in_=vn[b][:].rearrange("p t (c i) -> p c t i", i=4),
+            nc.gpsimd.tensor_scalar(
+                out=VG[b][:], in0=vn[b][:].rearrange("p t v -> p v t"), scalar1=1.0, scalar2=0.0, op0=ALU.mult, op1=ALU.add,
             )
 
         def quantise_v(b):
@@ -234,8 +245,8 @@ def tile_hyperbolicattention_t_kernel(tc, query, keys, values, c, out):
         def store(b):
             nc.sync.dma_start(out=out[b].rearrange("(p t) v -> p t v", t=NT), in_=OST[b][:])
 
-        order = {"act": [], "dve": [], "pe": [], "sp": []}
-        ring = {"P": [], "eT": [], "O": [], "qk": []}
+        order = {"act": [], "dve": [], "pe": [], "pool": [], "sp": []}
+        ring = {"P": [], "eT": [], "O": []}
 
         def add(eng, key, needs, fn):
             order[eng].append((key, [n for n in needs if n is not None], fn))
@@ -251,6 +262,12 @@ def tile_hyperbolicattention_t_kernel(tc, query, keys, values, c, out):
         def t_sq(b):
             add("act", ("sq", b), [("ldqk", chunk_of[b])], lambda: squares(b))
 
+        def t_sqmul(b):
+            add("dve", ("sqmul", b), [("ldqk", chunk_of[b]), ok("sq", b - 1)], lambda: square_mul(b))
+
+        def t_sqsum(b):
+            add("dve", ("sq", b), [("sqmul", b)], lambda: square_sum(b))
+
         def t_roots(b):
             add("act", ("roots", b), [("clamp", b, t) for t in range(NT)] + [ok("exps", b - GB)], lambda: roots(b))
 
@@ -263,48 +280,52 @@ def tile_hyperbolicattention_t_kernel(tc, query, keys, values, c, out):
         def t_const(ci):
             add("dve", ("const", ci), [("sq", b) for b in CHUNKS[ci]], lambda: constants(ci))
 
-        def t_prep_pe(b):
-            add("pe", ("tqk", b), [("ldqk", chunk_of[b]), back("qk", ("cqk", b), 1)], lambda: transpose_qk(b))
+        def t_tqk(b):
+            add("pe", ("tqk", b), [("ldqk", chunk_of[b]), back("P", ("cqk", b), NP_)], lambda: transpose_qk(b))
 
         def t_cqk(b):
-            add("dve", ("cqk", b), [("tqk", b), ok("cross", b - 2, NT - 1)], lambda: copy_qk(b))
+            add("dve", ("cqk", b), [("tqk", b)], lambda: copy_qk(b))
 
-        def t_cross(b):
-            for t in range(NT):
-                add("pe", ("cross", b, t), [("cqk", b), ("const", chunk_of[b]), back("P", ("clamp", b, t), NP_)], lambda t=t: cross(b, t))
+        def t_cross(b, tiles=(0, 1, 2, 3)):
+            if b < NB:
+                for t in tiles:
+                    add("pe", ("cross", b, t), [("cqk", b), ("const", chunk_of[b]), back("P", ("clamp", b, t), NP_)], lambda t=t: cross(b, t))
 
         def t_clamp(b):
-            for t in range(NT):
-                add("dve", ("clamp", b, t), [("cross", b, t), ok("add", b - GB)], lambda t=t: clamp(b, t))
+            if b < NB:
+                for t in range(NT):
+                    add("dve", ("clamp", b, t), [("cross", b, t), ok("add", b - GB)], lambda t=t: clamp(b, t))
 
         def t_add(b):
-            add("dve", ("add", b), [("roots", b)], lambda: add_roots(b))
+            add("pool", ("add", b), [("roots", b)], lambda: add_roots(b))
 
         def t_te(b):
-            for h in range(2):
-                add("pe", ("te", b, h), [("exps", b), back("eT", ("ce", b, h), NE_)], lambda h=h: transpose_e(b, h))
+            if b < NB:
+                for h in range(2):
+                    add("pe", ("te", b, h), [("exps", b), back("eT", ("ce", b, h), NE_)], lambda h=h: transpose_e(b, h))
 
         def t_ce(b, h, eng="dve"):
-            add(eng, ("ce", b, h), [("te", b, h), ok("qe", b - 2)], lambda: copy_e(b, h, eng))
+            add(eng, ("ce", b, h), [("te", b, h), ok("qe", b - 2), ("ce", b, 0) if h else None], lambda: copy_e(b, h, eng))
 
         def t_qe(b):
             add("dve", ("qe", b), [("ce", b, 0), ("ce", b, 1), ok("mx", b - 2, NT - 1)], lambda: quantise_e(b))
 
         def t_vr(b):
-            add("dve", ("vr", b), [("ldv", b), ok("vq", b - 2)], lambda: regroup_v(b))
+            add("pool", ("vr", b), [("ldv", b), ok("vq", b - GB)], lambda: regroup_v(b))
 
         def t_vq(b):
-            add("dve", ("vq", b), [("vr", b), ok("mx", b - NVC, NT - 1)], lambda: quantise_v(b))
+            if b < NB:
+                add("dve", ("vq", b), [("vr", b), ok("mx", b - NVC, NT - 1)], lambda: quantise_v(b))
 
-        def t_mx(b):
-            for t in range(NT):
+        def t_mx(b, tiles):
+            for t in tiles:
                 add("pe", ("mx", b, t), [("qe", b), ("vq", b), back("O", ("so", b, t), NO_)], lambda t=t: mx(b, t))
 
         def t_recip(b):
             add("dve", ("recip", b), [("exps", b)], lambda: recip(b))
 
         def t_so(b, t, eng="dve"):
-            add(eng, ("so", b, t), [("mx", b, t), ("recip", b), ok("st", b - 2)], lambda: scale_out(b, t, eng))
+            add(eng, ("so", b, t), [("mx", b, t), ("recip", b), ok("st", b - 2), ("so", b, 0) if t else None], lambda: scale_out(b, t, eng))
 
         def t_st(b):
             add("sp", ("st", b), [("so", b, t) for t in range(NT)], lambda: store(b))
@@ -316,109 +337,125 @@ def tile_hyperbolicattention_t_kernel(tc, query, keys, values, c, out):
         def t_ldqk(ci):
             add("sp", ("ldqk", ci), [], lambda: load_qk(ci))
 
-        for ci in (0, 1, 2):
+        for ci in (0, 1, 2, 3):
             t_ldqk(ci)
         t_ldv(0)
-        t_ldqk(3)
-        for b in (1, 2, 3):
-            t_ldv(b)
         t_ldqk(4)
         t_ldqk(5)
+        t_ldv(1)
+        t_ldv(2)
+        for b in range(GB):
+            t_ldv(b + NV)
+        for g in range(1, NG + 1):
+            f0 = (g - 1) * GB
+            t_st(f0)
+            t_st(f0 + 1)
+            t_ldv(g * GB + NV)
+            t_ldv(g * GB + NV + 1)
+            t_st(f0 + 2)
+            t_ldv(g * GB + NV + 2)
+            t_ldv(g * GB + NV + 3)
+            t_st(f0 + 3)
 
         t_sq(0)
         t_sq(1)
         for g in range(NG):
             for k in range(GB):
-                b = g * GB + k
-                t_roots(b)
-                if g == 0 and k < GB - 1:
-                    t_sq(2 * k + 2)
-                    t_sq(2 * k + 3)
+                t_roots(g * GB + k)
+                if g == 0 and k == 0:
+                    t_sq(2)
+                    t_sq(3)
             for k in range(GB):
                 t_logs(g * GB + k)
-                if g + 2 < NG:
-                    t_sq((g + 2) * GB + k)
             for k in range(GB):
                 t_exps(g * GB + k)
 
+        for g in range(NG):
+            for k in range(GB):
+                t_add(g * GB + k)
+            for k in range(GB):
+                t_vr(g * GB + k)
+
+        t_tqk(0)
+        t_tqk(1)
+        t_const(0)
+        t_cqk(0)
+        t_cqk(1)
         for b in range(GB):
-            t_prep_pe(b)
-            if b < 3:
-                t_const(b)
-            t_cqk(b)
             t_cross(b)
+            if b + 2 < GB:
+                t_tqk(b + 2)
             t_clamp(b)
-            if b >= 1:
-                t_add(b - 1)
-        t_vr(0)
-        t_add(GB - 1)
-        t_vq(0)
-        t_ldv(NV)
+            if b + 1 < 3:
+                t_const(b + 1)
+            if b + 2 < GB:
+                t_cqk(b + 2)
+        for b in range(GB, 2 * GB):
+            t_sqmul(b)
+            t_tqk(b)
+            t_cqk(b)
+            t_sqsum(b)
         t_const(3)
-        for k in range(1, GB):
-            nb = GB + k - 1
-            t_prep_pe(nb)
-            t_cqk(nb)
-            t_vr(k)
-            t_cross(nb)
-            t_vq(k)
-            t_ldv(NV + k)
-            t_clamp(nb)
+        for k in range(GB):
+            t_sqmul(2 * GB + k)
+            for b in range(2 * GB + 2 * k, 2 * GB + 2 * k + 2):
+                t_tqk(b)
+                t_cqk(b)
+            t_cross(GB + k)
+            t_sqsum(2 * GB + k)
+            if k < GB - 1:
+                t_clamp(GB + k)
         t_const(4)
+        t_vq(0)
+        t_te(0)
 
         for g in range(1, NG):
             for q in range(GB):
                 f = (g - 1) * GB + q
-                v = g * GB + q
                 r = g * GB + GB - 1 + q
-                if r < NB:
-                    t_prep_pe(r)
-                    t_cqk(r)
-                t_te(f)
+                s = 3 * GB + q if g == 1 else NB
+                if q < GB - 1:
+                    t_te(f + 1)
+                t_mx(f, (0, 1))
+                t_cross(r + 1, (0, 1, 2))
+                t_mx(f, (2, 3))
+                t_cross(r + 1, (3,))
+                if q == GB - 1:
+                    t_te(f + 1)
                 t_ce(f, 0)
                 t_ce(f, 1)
-                if q == 1:
-                    t_add(g * GB + 1)
-                if q == 2:
-                    t_add(g * GB + 3)
-                t_vr(v)
+                if s < NB:
+                    t_sqmul(s)
                 t_qe(f)
-                t_vq(v)
-                t_ldv(v + NV)
-                if r < NB:
-                    t_cross(r)
-                    t_clamp(r)
-                t_mx(f)
+                t_vq(f + 1)
+                if s < NB:
+                    t_sqsum(s)
+                t_clamp(r)
                 t_recip(f)
                 for t in range(NT):
                     t_so(f, t)
-                t_st(f)
-                if q == 0:
-                    t_add(g * GB)
-                if q == 1:
-                    t_add(g * GB + 2)
-            if g + 2 < NG:
-                t_const(g + 4)
+            if g == 1:
+                t_const(5)
 
         for q in range(GB):
             f = (NG - 1) * GB + q
             shared = q >= 2
-            t_te(f)
+            t_te(f + 1)
+            t_mx(f, (0, 1, 2, 3))
             t_ce(f, 0)
             t_ce(f, 1, "act" if shared else "dve")
             t_recip(f)
             t_qe(f)
-            t_mx(f)
+            t_vq(f + 1)
             for t in range(NT):
                 t_so(f, t, "act" if (shared and t % 2 == 1) else "dve")
-            t_st(f)
 
         done = set()
         at = {e: 0 for e in order}
         left = sum(len(v) for v in order.values())
         while left:
             moved = 0
-            for e in ("sp", "act", "pe", "dve"):
+            for e in ("sp", "act", "pe", "pool", "dve"):
                 while at[e] < len(order[e]) and all(n in done for n in order[e][at[e]][1]):
                     key, needs, fn = order[e][at[e]]
                     fn()

@@ -28,7 +28,6 @@ CHUNKS = ((0,), (1,), (2, 3), (4, 5, 6, 7), (8, 9, 10, 11), (12, 13, 14, 15))
 NV = 3
 NVC = 3
 NP_, NE_, NO_ = 4, 2, 2
-ACT_SQUARES = GB
 G2N, B0, B1, HI, NK2H = 4, 5, 6, 7, 8
 
 
@@ -174,7 +173,8 @@ def tile_hyperbolicattention_t_kernel(tc, query, keys, values, c, out):
                 nc.scalar.activation(out=X[b][:, t, 0:W1], in_=X[b][:, t, 0:W1], func=AF.Sqrt, bias=cst(b, t, B0), scale=cst(b, t, G2N))
 
         def add_roots(b):
-            nc.gpsimd.tensor_tensor(out=R[b][:, :, 0:W1], in0=R[b][:, :, 0:W1], in1=X[b][:, :, 0:W1], op=ALU.add)
+            for t in range(NT):
+                nc.gpsimd.tensor_tensor(out=R[b][:, t, 0:W1], in0=R[b][:, t, 0:W1], in1=X[b][:, t, 0:W1], op=ALU.add)
 
         def logs(b):
             nc.scalar.activation(out=R[b][:, :, 0:W1], in_=R[b][:, :, 0:W1], func=AF.Ln)
@@ -217,9 +217,12 @@ def tile_hyperbolicattention_t_kernel(tc, query, keys, values, c, out):
 
         def regroup_v(b):
             VG[b] = vgp.tile([P, DV, NT], BF16, name="vg", align_bytes=64)
-            nc.gpsimd.tensor_scalar(
-                out=VG[b][:], in0=vn[b][:].rearrange("p t v -> p v t"), scalar1=1.0, scalar2=0.0, op0=ALU.mult, op1=ALU.add,
-            )
+            for k in range(NT):
+                cols = slice(k * P, (k + 1) * P)
+                nc.gpsimd.tensor_scalar(
+                    out=VG[b][:, cols, :], in0=vn[b][:, :, cols].rearrange("p t v -> p v t"),
+                    scalar1=1.0, scalar2=0.0, op0=ALU.mult, op1=ALU.add,
+                )
 
         def quantise_v(b):
             VC[b] = vcp.tile([P, DV], U32, name="vc", align_bytes=64)

@@ -26,7 +26,7 @@ GB = 4
 NG = NB // GB
 CHUNKS = ((0,), (1,), (2, 3), (4, 5, 6, 7), (8, 9, 10, 11), (12, 13, 14, 15))
 NV = 3
-NVC = 3
+NVC = 4
 NP_, NE_, NO_ = 4, 2, 2
 G2N, B0, B1, HI, NK2H = 4, 5, 6, 7, 8
 
@@ -51,6 +51,7 @@ def tile_hyperbolicattention_t_kernel(tc, query, keys, values, c, out):
         ps_e = ctx.enter_context(tc.psum_pool(name="ps_e", bufs=NE_))
         ps_o = ctx.enter_context(tc.psum_pool(name="ps_o", bufs=NO_))
 
+        psum_of = {"P": ps_p, "eT": ps_e, "O": ps_o}
         chunk_of = {}
         for ci, ch in enumerate(CHUNKS):
             for b in ch:
@@ -194,8 +195,8 @@ def tile_hyperbolicattention_t_kernel(tc, query, keys, values, c, out):
             RI[b] = smallp.tile([P, NT], F32, name="ri")
             nc.vector.reciprocal(out=RI[b][:], in_=RS[b][:])
 
-        def transpose_e(b, h):
-            ET[b, h] = ps_e.tile([P, 2, NT, P], BF16, name="eT")
+        def transpose_e(b, h, ring_name):
+            ET[b, h] = psum_of[ring_name].tile([P, 2, NT, P], BF16, name=ring_name)
             for a in range(2):
                 for tj in range(NT):
                     nc.tensor.transpose(ET[b, h][:, a, tj, :], E[b][:, 2 * h + a, tj * P : (tj + 1) * P], ident_bf[:])
@@ -229,8 +230,8 @@ def tile_hyperbolicattention_t_kernel(tc, query, keys, values, c, out):
             VS[b] = vcp.tile([P, DV], U8, name="vs", align_bytes=64)
             nc.vector.quantize_mx(out=VC[b][:].bitcast(FP8X4), scales=VS[b][:], in_=VG[b][:].rearrange("p v t -> p (v t)"))
 
-        def mx(b, t):
-            O[b, t] = ps_o.tile([P, DV], F32, name="O")
+        def mx(b, t, ring_name):
+            O[b, t] = psum_of[ring_name].tile([P, DV], F32, name=ring_name)
             cols = slice(t * P, (t + 1) * P)
             nc.tensor.matmul_mx(
                 out=O[b, t][:], lhsT=EC[b][:, cols].bitcast(FP8X4), lhsT_scale=ES[b][:, cols],
@@ -238,18 +239,19 @@ def tile_hyperbolicattention_t_kernel(tc, query, keys, values, c, out):
             )
 
         def scale_out(b, t, eng):
-            if t == 0:
+            if b not in OST:
                 OST[b] = ostp.tile([P, NT, DV], F32, name="ost")
             if eng == "act":
                 nc.scalar.activation(out=OST[b][:, t, :], in_=O[b, t][:], func=AF.Copy, scale=RI[b][:, t : t + 1])
             else:
                 nc.vector.tensor_scalar_mul(out=OST[b][:, t, :], in0=O[b, t][:], scalar1=RI[b][:, t : t + 1])
 
-        def store(b):
-            nc.sync.dma_start(out=out[b].rearrange("(p t) v -> p t v", t=NT), in_=OST[b][:])
+        def store(b, tiles):
+            nc.sync.dma_start(out=out[b].rearrange("(p t) v -> p t v", t=NT)[:, tiles, :], in_=OST[b][:, tiles, :])
 
         order = {"act": [], "dve": [], "pe": [], "pool": [], "sp": []}
         ring = {"P": [], "eT": [], "O": []}
+        depth_of = {"P": NP_, "eT": NE_, "O": NO_}
 
         def add(eng, key, needs, fn):
             order[eng].append((key, [n for n in needs if n is not None], fn))
@@ -302,10 +304,11 @@ def tile_hyperbolicattention_t_kernel(tc, query, keys, values, c, out):
         def t_add(b):
             add("pool", ("add", b), [("roots", b)], lambda: add_roots(b))
 
-        def t_te(b):
+        def t_te(b, ring_name="eT"):
             if b < NB:
                 for h in range(2):
-                    add("pe", ("te", b, h), [("exps", b), back("eT", ("ce", b, h), NE_)], lambda h=h: transpose_e(b, h))
+                    freed = back(ring_name, ("ce", b, h), depth_of[ring_name])
+                    add("pe", ("te", b, h), [("exps", b), freed], lambda h=h: transpose_e(b, h, ring_name))
 
         def t_ce(b, h, eng="dve"):
             add(eng, ("ce", b, h), [("te", b, h), ok("qe", b - 2), ("ce", b, 0) if h else None], lambda: copy_e(b, h, eng))
@@ -320,18 +323,23 @@ def tile_hyperbolicattention_t_kernel(tc, query, keys, values, c, out):
             if b < NB:
                 add("dve", ("vq", b), [("vr", b), ok("mx", b - NVC, NT - 1)], lambda: quantise_v(b))
 
-        def t_mx(b, tiles):
+        def t_mx(b, tiles, ring_name="O"):
             for t in tiles:
-                add("pe", ("mx", b, t), [("qe", b), ("vq", b), back("O", ("so", b, t), NO_)], lambda t=t: mx(b, t))
+                freed = back(ring_name, ("so", b, t), depth_of[ring_name])
+                add("pe", ("mx", b, t), [("qe", b), ("vq", b), freed], lambda t=t: mx(b, t, ring_name))
 
         def t_recip(b):
             add("dve", ("recip", b), [("exps", b)], lambda: recip(b))
 
         def t_so(b, t, eng="dve"):
-            add(eng, ("so", b, t), [("mx", b, t), ("recip", b), ok("st", b - 2), ("so", b, 0) if t else None], lambda: scale_out(b, t, eng))
+            add(eng, ("so", b, t), [("mx", b, t), ("recip", b), ok("st", b - 2)], lambda: scale_out(b, t, eng))
 
         def t_st(b):
-            add("sp", ("st", b), [("so", b, t) for t in range(NT)], lambda: store(b))
+            add("sp", ("st", b), [("so", b, t) for t in range(NT)], lambda: store(b, slice(0, NT)))
+
+        def t_st_half(b, h, last):
+            key = ("st", b) if last else ("st_first", b)
+            add("sp", key, [("so", b, 2 * h), ("so", b, 2 * h + 1)], lambda: store(b, slice(2 * h, 2 * h + 2)))
 
         def t_ldv(b):
             if b < NB:
@@ -349,7 +357,7 @@ def tile_hyperbolicattention_t_kernel(tc, query, keys, values, c, out):
         t_ldv(2)
         for b in range(GB):
             t_ldv(b + NV)
-        for g in range(1, NG + 1):
+        for g in range(1, NG):
             f0 = (g - 1) * GB
             t_st(f0)
             t_st(f0 + 1)
@@ -359,6 +367,9 @@ def tile_hyperbolicattention_t_kernel(tc, query, keys, values, c, out):
             t_ldv(g * GB + NV + 2)
             t_ldv(g * GB + NV + 3)
             t_st(f0 + 3)
+        for f in range(NB - GB, NB):
+            t_st_half(f, 1, False)
+            t_st_half(f, 0, True)
 
         t_sq(0)
         t_sq(1)
@@ -427,6 +438,9 @@ def tile_hyperbolicattention_t_kernel(tc, query, keys, values, c, out):
                     t_te(f + 1)
                 t_ce(f, 0)
                 t_ce(f, 1)
+                if f > 0:
+                    t_so(f - 1, 2)
+                    t_so(f - 1, 3)
                 if s < NB:
                     t_sqmul(s)
                 t_qe(f)
@@ -435,23 +449,50 @@ def tile_hyperbolicattention_t_kernel(tc, query, keys, values, c, out):
                     t_sqsum(s)
                 t_clamp(r)
                 t_recip(f)
-                for t in range(NT):
-                    t_so(f, t)
+                t_so(f, 0)
+                t_so(f, 1)
             if g == 1:
                 t_const(5)
 
-        for q in range(GB):
-            f = (NG - 1) * GB + q
-            shared = q >= 2
-            t_te(f + 1)
-            t_mx(f, (0, 1, 2, 3))
+        l0 = NB - GB
+        t_te(l0 + 1, "P")
+        t_mx(l0, (0, 1))
+        t_mx(l0, (2, 3), "P")
+        t_te(l0 + 2)
+        t_mx(l0 + 1, (2, 3), "P")
+        t_mx(l0 + 1, (0, 1))
+        t_te(l0 + 3, "P")
+        t_mx(l0 + 2, (2, 3), "P")
+        t_mx(l0 + 2, (0, 1))
+        t_mx(l0 + 3, (2, 3), "P")
+        t_mx(l0 + 3, (0, 1), "eT")
+
+        t_vq(l0 + 1)
+        for f in (l0, l0 + 1):
             t_ce(f, 0)
-            t_ce(f, 1, "act" if shared else "dve")
+            t_ce(f, 1)
+            if f == l0:
+                t_so(f - 1, 2)
+                t_so(f - 1, 3)
             t_recip(f)
             t_qe(f)
-            t_vq(f + 1)
-            for t in range(NT):
-                t_so(f, t, "act" if (shared and t % 2 == 1) else "dve")
+            t_vq(f + 2)
+        for f in (l0 + 2, l0 + 3):
+            t_so(f - 2, 0)
+            t_so(f - 2, 1)
+            t_ce(f, 0)
+            t_recip(f)
+            t_qe(f)
+        for f in (l0 + 2, l0 + 3):
+            t_so(f, 0)
+            t_so(f, 1)
+        for f in (l0, l0 + 1):
+            t_so(f, 2, "act")
+            t_so(f, 3, "act")
+            t_ce(f + 2, 1, "act")
+        for f in (l0 + 2, l0 + 3):
+            t_so(f, 2, "act")
+            t_so(f, 3, "act")
 
         done = set()
         at = {e: 0 for e in order}

@@ -27,7 +27,7 @@ NG = NB // GB
 CHUNKS = ((0,), (1,), (2, 3), (4, 5, 6, 7), (8, 9, 10, 11), (12, 13, 14, 15))
 NV = 3
 NVC = 4
-NP_, NE_, NO_ = 4, 2, 2
+NP_, NE_, NO_ = 2, 2, 4
 G2N, B0, B1, HI, NK2H = 4, 5, 6, 7, 8
 
 
@@ -119,6 +119,21 @@ def tile_hyperbolicattention_t_kernel(tc, query, keys, values, c, out):
                 axis=mybir.AxisListType.X, op=ALU.add,
             )
 
+        def square_piece(b, k):
+            ci = chunk_of[b]
+            w = k % 2
+            if k == 0:
+                SQF[b] = sqfp.tile([P, 2 * S], F32, name="sqf")
+            half = SQF[b][:, w * S : (w + 1) * S]
+            if k < 2:
+                src = qk[ci][:, b - CHUNKS[ci][0], w, :]
+                nc.vector.tensor_tensor(out=half, in0=src, in1=src, op=ALU.mult)
+            else:
+                nc.vector.tensor_reduce(
+                    out=sq[ci][:, w, col(b, 0) : col(b, 0) + NT], in_=half.rearrange("p (t d) -> p t d", t=NT),
+                    axis=mybir.AxisListType.X, op=ALU.add,
+                )
+
         def constants(ci):
             n = NT * len(CHUNKS[ci])
             t_ = const.tile([P, 9, n], F32, name="cs%d" % ci)
@@ -140,7 +155,7 @@ def tile_hyperbolicattention_t_kernel(tc, query, keys, values, c, out):
             return cs[chunk_of[b]][:, row, col(b, t) : col(b, t) + 1]
 
         def transpose_qk(b):
-            qkps[b] = ps_p.tile([P, 2 * S], BF16, name="P")
+            qkps[b] = ps_o.tile([P, 2 * S], BF16, name="O")
             for w in range(2):
                 for t in range(NT):
                     nc.tensor.transpose(qkps[b][:, w * S + t * P : w * S + (t + 1) * P], rows_of(w, b, t), ident_bf[:])
@@ -149,8 +164,8 @@ def tile_hyperbolicattention_t_kernel(tc, query, keys, values, c, out):
             qkT[b] = const.tile([P, 2 * S], BF16, name="qkT%d" % b)
             nc.vector.tensor_copy(out=qkT[b][:], in_=qkps[b][:])
 
-        def cross(b, t):
-            ps = ps_p.tile([P, S], F32, name="P")
+        def cross(b, t, ring_name):
+            ps = psum_of[ring_name].tile([P, S], F32, name=ring_name)
             PS[b, t] = ps
             nc.tensor.matmul(out=ps[:], lhsT=qkT[b][:, t * P : (t + 1) * P], rhs=qkT[b][:, S : 2 * S], start=True, stop=False)
             for tj in range(NT):
@@ -273,6 +288,11 @@ def tile_hyperbolicattention_t_kernel(tc, query, keys, values, c, out):
         def t_sqsum(b):
             add("dve", ("sq", b), [("sqmul", b)], lambda: square_sum(b))
 
+        def t_sqpiece(b, k):
+            key = ("sq", b) if k == 3 else ("sqpiece", b, k)
+            before = ("sqpiece", b, k - 1) if k else (("sq", b - 1) if b > GB else None)
+            add("dve", key, [("ldqk", chunk_of[b]), before], lambda: square_piece(b, k))
+
         def t_roots(b):
             add("act", ("roots", b), [("clamp", b, t) for t in range(NT)] + [ok("exps", b - GB)], lambda: roots(b))
 
@@ -286,20 +306,23 @@ def tile_hyperbolicattention_t_kernel(tc, query, keys, values, c, out):
             add("dve", ("const", ci), [("sq", b) for b in CHUNKS[ci]], lambda: constants(ci))
 
         def t_tqk(b):
-            add("pe", ("tqk", b), [("ldqk", chunk_of[b]), back("P", ("cqk", b), NP_)], lambda: transpose_qk(b))
+            add("pe", ("tqk", b), [("ldqk", chunk_of[b]), back("O", ("cqk", b), NO_)], lambda: transpose_qk(b))
 
         def t_cqk(b):
             add("dve", ("cqk", b), [("tqk", b)], lambda: copy_qk(b))
 
-        def t_cross(b, tiles=(0, 1, 2, 3)):
+        def t_cross(b, tiles, ring_name="P"):
             if b < NB:
                 for t in tiles:
-                    add("pe", ("cross", b, t), [("cqk", b), ("const", chunk_of[b]), back("P", ("clamp", b, t), NP_)], lambda t=t: cross(b, t))
+                    freed = back(ring_name, ("clamp", b, t), depth_of[ring_name])
+                    add("pe", ("cross", b, t), [("cqk", b), ("const", chunk_of[b]), freed], lambda t=t: cross(b, t, ring_name))
 
-        def t_clamp(b):
+        def t_clamp(b, tiles=(0, 1, 2, 3), squares_of=None):
             if b < NB:
-                for t in range(NT):
+                for t in tiles:
                     add("dve", ("clamp", b, t), [("cross", b, t), ok("add", b - GB)], lambda t=t: clamp(b, t))
+                    if squares_of is not None:
+                        t_sqpiece(squares_of, t)
 
         def t_add(b):
             add("pool", ("add", b), [("roots", b)], lambda: add_roots(b))
@@ -396,26 +419,29 @@ def tile_hyperbolicattention_t_kernel(tc, query, keys, values, c, out):
         t_cqk(0)
         t_cqk(1)
         for b in range(GB):
-            t_cross(b)
+            t_cross(b, (0, 1, 2, 3), "O")
             if b + 2 < GB:
                 t_tqk(b + 2)
-            t_clamp(b)
+            t_clamp(b, squares_of=GB + b - 1 if b else None)
             if b + 1 < 3:
                 t_const(b + 1)
             if b + 2 < GB:
                 t_cqk(b + 2)
+        for k in range(4):
+            t_sqpiece(2 * GB - 1, k)
+        t_const(3)
         for b in range(GB, 2 * GB):
-            t_sqmul(b)
             t_tqk(b)
             t_cqk(b)
-            t_sqsum(b)
-        t_const(3)
         for k in range(GB):
             t_sqmul(2 * GB + k)
             for b in range(2 * GB + 2 * k, 2 * GB + 2 * k + 2):
                 t_tqk(b)
                 t_cqk(b)
-            t_cross(GB + k)
+            if k < GB - 1:
+                t_cross(GB + k, (0, 1, 2, 3), "O")
+            else:
+                t_cross(GB + k, (0, 1))
             t_sqsum(2 * GB + k)
             if k < GB - 1:
                 t_clamp(GB + k)
@@ -430,50 +456,40 @@ def tile_hyperbolicattention_t_kernel(tc, query, keys, values, c, out):
                 s = 3 * GB + q if g == 1 else NB
                 if q < GB - 1:
                     t_te(f + 1)
-                t_mx(f, (0, 1))
-                t_cross(r + 1, (0, 1, 2))
-                t_mx(f, (2, 3))
-                t_cross(r + 1, (3,))
+                t_cross(r, (2, 3))
+                t_mx(f, (0, 1, 2, 3))
+                t_cross(r + 1, (0, 1))
                 if q == GB - 1:
                     t_te(f + 1)
                 t_ce(f, 0)
                 t_ce(f, 1)
-                if f > 0:
-                    t_so(f - 1, 2)
-                    t_so(f - 1, 3)
+                t_clamp(r, (0, 1))
                 if s < NB:
                     t_sqmul(s)
                 t_qe(f)
                 t_vq(f + 1)
                 if s < NB:
                     t_sqsum(s)
-                t_clamp(r)
+                t_clamp(r, (2, 3))
                 t_recip(f)
-                t_so(f, 0)
-                t_so(f, 1)
+                for t in range(NT):
+                    t_so(f, t)
             if g == 1:
                 t_const(5)
 
         l0 = NB - GB
         t_te(l0 + 1, "P")
-        t_mx(l0, (0, 1))
-        t_mx(l0, (2, 3), "P")
+        t_mx(l0, (0, 1, 2, 3))
         t_te(l0 + 2)
-        t_mx(l0 + 1, (2, 3), "P")
-        t_mx(l0 + 1, (0, 1))
+        t_mx(l0 + 1, (0, 1, 2, 3))
         t_te(l0 + 3, "P")
-        t_mx(l0 + 2, (2, 3), "P")
-        t_mx(l0 + 2, (0, 1))
-        t_mx(l0 + 3, (2, 3), "P")
-        t_mx(l0 + 3, (0, 1), "eT")
+        t_mx(l0 + 2, (0, 1, 2, 3))
+        t_mx(l0 + 3, (0, 1, 2, 3))
 
         t_vq(l0 + 1)
         for f in (l0, l0 + 1):
             t_ce(f, 0)
             t_ce(f, 1)
-            if f == l0:
-                t_so(f - 1, 2)
-                t_so(f - 1, 3)
             t_recip(f)
             t_qe(f)
             t_vq(f + 2)

@@ -23,7 +23,11 @@ WP = S + 8
 FLOPS = 2 * NB * S * S * (D + DV)
 
 GB = 4
-NG = NB // GB
+GROUPS = ((0, 1, 2, 3), (4, 5, 6, 7, 8), (9, 10, 11, 12, 13), (14, 15))
+GMAX = 5
+NX = 4
+NVG = 4
+AHEAD = 7
 CHUNKS = ((0,), (1,), (2, 3), (4, 5, 6, 7), (8, 9, 10, 11), (12, 13, 14, 15))
 NV = 3
 NVC = 4
@@ -37,14 +41,14 @@ def tile_hyperbolicattention_t_kernel(tc, query, keys, values, c, out):
         ctx.enter_context(tc.manual_schedule())
         const = ctx.enter_context(tc.tile_pool(name="const", bufs=1))
         sqfp = ctx.enter_context(tc.tile_pool(name="sqfp", bufs=1))
-        xp = ctx.enter_context(tc.tile_pool(name="xp", bufs=GB))
-        rp = ctx.enter_context(tc.tile_pool(name="rp", bufs=GB))
-        smallp = ctx.enter_context(tc.tile_pool(name="smallp", bufs=2 * GB))
-        ep = ctx.enter_context(tc.tile_pool(name="ep", bufs=GB))
+        xp = ctx.enter_context(tc.tile_pool(name="xp", bufs=NX))
+        rp = ctx.enter_context(tc.tile_pool(name="rp", bufs=GMAX))
+        smallp = ctx.enter_context(tc.tile_pool(name="smallp", bufs=2 * GMAX))
+        ep = ctx.enter_context(tc.tile_pool(name="ep", bufs=GMAX))
         grpp = ctx.enter_context(tc.tile_pool(name="grpp", bufs=2))
         ecp = ctx.enter_context(tc.tile_pool(name="ecp", bufs=2))
         vnp = ctx.enter_context(tc.tile_pool(name="vnp", bufs=NV))
-        vgp = ctx.enter_context(tc.tile_pool(name="vgp", bufs=GB))
+        vgp = ctx.enter_context(tc.tile_pool(name="vgp", bufs=NVG))
         vcp = ctx.enter_context(tc.tile_pool(name="vcp", bufs=NVC))
         ostp = ctx.enter_context(tc.tile_pool(name="ostp", bufs=2))
         ps_p = ctx.enter_context(tc.psum_pool(name="ps_p", bufs=NP_))
@@ -70,7 +74,7 @@ def tile_hyperbolicattention_t_kernel(tc, query, keys, values, c, out):
         nc.vector.memset(one[:], 1.0)
         warm = const.tile([P, 1], F32, name="warm")
         nc.scalar.activation(out=warm[:], in_=one[:], func=AF.Sqrt)
-        junk = const.tile([P, D], BF16, name="junk")
+        junk = const.tile([P, 2 * NT, D], BF16, name="junk")
         cc = const.tile([P, 8], F32, name="cc")
         cf, negc, neg2c, rc, e4c = (cc[:, i : i + 1] for i in range(5))
         nc.vector.tensor_copy(out=cf, in_=c_bf[:])
@@ -99,10 +103,10 @@ def tile_hyperbolicattention_t_kernel(tc, query, keys, values, c, out):
             nc.sync.dma_start(out=vn[b][:], in_=values[b].rearrange("(p t) v -> p t v", t=NT))
 
         def squares(b):
-            for w in range(2):
+            for w in (1, 0):
                 for t in range(NT):
                     nc.scalar.activation(
-                        out=junk[:], in_=rows_of(w, b, t), func=AF.Square,
+                        out=junk[:, w * NT + t, :], in_=rows_of(w, b, t), func=AF.Square,
                         accum_out=sq[chunk_of[b]][:, w, col(b, t) : col(b, t) + 1],
                     )
 
@@ -139,16 +143,16 @@ def tile_hyperbolicattention_t_kernel(tc, query, keys, values, c, out):
             t_ = const.tile([P, 9, n], F32, name="cs%d" % ci)
             cs[ci] = t_
             q2, k2 = sq[ci][:, 0, :], sq[ci][:, 1, :]
+            nc.vector.tensor_scalar_mul(out=t_[:, NK2H, :], in0=k2, scalar1=-0.5)
             nc.vector.tensor_scalar(out=t_[:, 0:2, :], in0=sq[ci][:], scalar1=negc, scalar2=1.0, op0=ALU.mult, op1=ALU.add)
             den = t_[:, 2, :]
             nc.vector.tensor_tensor(out=den, in0=t_[:, 0, :], in1=t_[:, 1, :], op=ALU.mult)
             nc.vector.tensor_scalar_max(out=den, in0=den, scalar1=EPS)
-            nc.vector.reciprocal(out=t_[:, 3, :], in_=den)
-            nc.vector.tensor_scalar(out=t_[:, G2N, :], in0=t_[:, 3, :], scalar1=neg2c, scalar2=None, op0=ALU.mult)
-            nc.vector.tensor_scalar_mul(out=t_[:, NK2H, :], in0=k2, scalar1=-0.5)
             nc.vector.tensor_scalar(out=t_[:, 0, :], in0=den, scalar1=e4c, scalar2=None, op0=ALU.mult)
+            nc.vector.reciprocal(out=t_[:, 3, :], in_=den)
             nc.vector.scalar_tensor_tensor(out=t_[:, HI, :], in0=q2, scalar=(1.0 - KAPPA) / 2.0, in1=t_[:, 0, :], op0=ALU.mult, op1=ALU.subtract)
-            nc.vector.scalar_tensor_tensor(out=t_[:, B0, :], in0=t_[:, G2N, :], scalar=-0.5, in1=q2, op0=ALU.mult, op1=ALU.mult)
+            nc.vector.tensor_scalar(out=t_[:, G2N, :], in0=t_[:, 3, :], scalar1=neg2c, scalar2=None, op0=ALU.mult)
+            nc.vector.scalar_tensor_tensor(out=t_[:, B0, :], in0=t_[:, 3, :], scalar=cf, in1=q2, op0=ALU.mult, op1=ALU.mult)
             nc.vector.tensor_scalar_add(out=t_[:, B1, :], in0=t_[:, B0, :], scalar1=1.0)
 
         def cst(b, t, row):
@@ -184,9 +188,12 @@ def tile_hyperbolicattention_t_kernel(tc, query, keys, values, c, out):
 
         def roots(b):
             R[b] = rp.tile([P, NT, WP], F32, name="R")
-            for t in range(NT):
-                nc.scalar.activation(out=R[b][:, t, 0:W1], in_=X[b][:, t, 0:W1], func=AF.Sqrt, bias=cst(b, t, B1), scale=cst(b, t, G2N))
-                nc.scalar.activation(out=X[b][:, t, 0:W1], in_=X[b][:, t, 0:W1], func=AF.Sqrt, bias=cst(b, t, B0), scale=cst(b, t, G2N))
+            for t in range(NT + 1):
+                if t < NT:
+                    nc.scalar.activation(out=R[b][:, t, 0:W1], in_=X[b][:, t, 0:W1], func=AF.Sqrt, bias=cst(b, t, B1), scale=cst(b, t, G2N))
+                if t > 0:
+                    u = t - 1
+                    nc.scalar.activation(out=X[b][:, u, 0:W1], in_=X[b][:, u, 0:W1], func=AF.Sqrt, bias=cst(b, u, B0), scale=cst(b, u, G2N))
 
         def add_roots(b):
             for t in range(NT):
@@ -194,8 +201,12 @@ def tile_hyperbolicattention_t_kernel(tc, query, keys, values, c, out):
 
         def logs(b):
             nc.scalar.activation(out=R[b][:, :, 0:W1], in_=R[b][:, :, 0:W1], func=AF.Ln)
+
+        def exp_bias(b):
             EB[b] = smallp.tile([P, NT], F32, name="eb")
-            nc.scalar.mul(out=EB[b][:].unsqueeze(2), in_=R[b][:, :, S:W1], mul=INV_SCALE2)
+            nc.gpsimd.tensor_scalar(
+                out=EB[b][:].unsqueeze(2), in0=R[b][:, :, S:W1], scalar1=INV_SCALE2, scalar2=0.0, op0=ALU.mult, op1=ALU.add,
+            )
 
         def exps(b):
             E[b] = ep.tile([P, NT, S], BF16, name="e")
@@ -294,13 +305,16 @@ def tile_hyperbolicattention_t_kernel(tc, query, keys, values, c, out):
             add("dve", key, [("ldqk", chunk_of[b]), before], lambda: square_piece(b, k))
 
         def t_roots(b):
-            add("act", ("roots", b), [("clamp", b, t) for t in range(NT)] + [ok("exps", b - GB)], lambda: roots(b))
+            add("act", ("roots", b), [("clamp", b, t) for t in range(NT)] + [ok("exps", b - GMAX)], lambda: roots(b))
 
         def t_logs(b):
             add("act", ("logs", b), [("add", b)], lambda: logs(b))
 
         def t_exps(b):
-            add("act", ("exps", b), [("logs", b), ok("te", b - GB, 1)], lambda: exps(b))
+            add("act", ("exps", b), [("eb", b), ok("te", b - GMAX, 1)], lambda: exps(b))
+
+        def t_eb(b):
+            add("pool", ("eb", b), [("logs", b)], lambda: exp_bias(b))
 
         def t_const(ci):
             add("dve", ("const", ci), [("sq", b) for b in CHUNKS[ci]], lambda: constants(ci))
@@ -320,7 +334,7 @@ def tile_hyperbolicattention_t_kernel(tc, query, keys, values, c, out):
         def t_clamp(b, tiles=(0, 1, 2, 3), squares_of=None):
             if b < NB:
                 for t in tiles:
-                    add("dve", ("clamp", b, t), [("cross", b, t), ok("add", b - GB)], lambda t=t: clamp(b, t))
+                    add("dve", ("clamp", b, t), [("cross", b, t), ok("add", b - NX)], lambda t=t: clamp(b, t))
                     if squares_of is not None:
                         t_sqpiece(squares_of, t)
 
@@ -340,7 +354,7 @@ def tile_hyperbolicattention_t_kernel(tc, query, keys, values, c, out):
             add("dve", ("qe", b), [("ce", b, 0), ("ce", b, 1), ok("mx", b - 2, NT - 1)], lambda: quantise_e(b))
 
         def t_vr(b):
-            add("pool", ("vr", b), [("ldv", b), ok("vq", b - GB)], lambda: regroup_v(b))
+            add("pool", ("vr", b), [("ldv", b), ok("vq", b - NVG)], lambda: regroup_v(b))
 
         def t_vq(b):
             if b < NB:
@@ -380,43 +394,43 @@ def tile_hyperbolicattention_t_kernel(tc, query, keys, values, c, out):
         t_ldv(2)
         for b in range(GB):
             t_ldv(b + NV)
-        for g in range(1, NG):
-            f0 = (g - 1) * GB
-            t_st(f0)
-            t_st(f0 + 1)
-            t_ldv(g * GB + NV)
-            t_ldv(g * GB + NV + 1)
-            t_st(f0 + 2)
-            t_ldv(g * GB + NV + 2)
-            t_ldv(g * GB + NV + 3)
-            t_st(f0 + 3)
-        for f in range(NB - GB, NB):
+        for gi in range(1, len(GROUPS)):
+            loads = [b + NV for b in GROUPS[gi]]
+            for k, f in enumerate(GROUPS[gi - 1]):
+                t_st(f)
+                if k >= 1:
+                    for b in loads[2 * k - 2 : 2 * k]:
+                        t_ldv(b)
+            for b in loads[2 * len(GROUPS[gi - 1]) - 2 :]:
+                t_ldv(b)
+        for f in GROUPS[-1]:
             t_st_half(f, 1, False)
             t_st_half(f, 0, True)
 
         t_sq(0)
         t_sq(1)
-        for g in range(NG):
-            for k in range(GB):
-                t_roots(g * GB + k)
-                if g == 0 and k == 0:
+        for group in GROUPS:
+            for b in group:
+                t_roots(b)
+                if b == 0:
                     t_sq(2)
                     t_sq(3)
-            for k in range(GB):
-                t_logs(g * GB + k)
-            for k in range(GB):
-                t_exps(g * GB + k)
+            for b in group:
+                t_logs(b)
+            for b in group:
+                t_exps(b)
 
-        for g in range(NG):
-            for k in range(GB):
-                t_add(g * GB + k)
-            for k in range(GB):
-                t_vr(g * GB + k)
+        for group in GROUPS:
+            for b in group:
+                t_add(b)
+            for b in group:
+                t_vr(b)
+                t_eb(b)
 
         t_tqk(0)
         t_tqk(1)
-        t_const(0)
         t_cqk(0)
+        t_const(0)
         t_cqk(1)
         for b in range(GB):
             t_cross(b, (0, 1, 2, 3), "O")
@@ -449,66 +463,70 @@ def tile_hyperbolicattention_t_kernel(tc, query, keys, values, c, out):
         t_vq(0)
         t_te(0)
 
-        for g in range(1, NG):
-            for q in range(GB):
-                f = (g - 1) * GB + q
-                r = g * GB + GB - 1 + q
-                s = 3 * GB + q if g == 1 else NB
-                if q < GB - 1:
-                    t_te(f + 1)
-                t_cross(r, (2, 3))
-                t_mx(f, (0, 1, 2, 3))
-                t_cross(r + 1, (0, 1))
-                if q == GB - 1:
-                    t_te(f + 1)
-                t_ce(f, 0)
-                t_ce(f, 1)
-                t_clamp(r, (0, 1))
-                if s < NB:
-                    t_sqmul(s)
-                t_qe(f)
-                t_vq(f + 1)
-                if s < NB:
-                    t_sqsum(s)
-                t_clamp(r, (2, 3))
-                t_recip(f)
-                for t in range(NT):
-                    t_so(f, t)
-            if g == 1:
-                t_const(5)
-
-        l0 = NB - GB
-        t_te(l0 + 1, "P")
-        t_mx(l0, (0, 1, 2, 3))
-        t_te(l0 + 2)
-        t_mx(l0 + 1, (0, 1, 2, 3))
-        t_te(l0 + 3, "P")
-        t_mx(l0 + 2, (0, 1, 2, 3))
-        t_mx(l0 + 3, (0, 1, 2, 3))
-
-        t_vq(l0 + 1)
-        for f in (l0, l0 + 1):
+        ends = [group[-1] for group in GROUPS]
+        last = GROUPS[-1]
+        n = len(last)
+        for f in range(last[0]):
+            r = f + AHEAD
+            late = 3 * GB + f if f < GB else NB
+            if f not in ends:
+                t_te(f + 1)
+            t_cross(r, (2, 3))
+            t_mx(f, (0, 1, 2, 3))
+            t_cross(r + 1, (0, 1))
+            if f in ends:
+                t_te(f + 1)
             t_ce(f, 0)
             t_ce(f, 1)
+            t_clamp(r, (0, 1))
             t_recip(f)
+            if late < NB:
+                t_sqmul(late)
             t_qe(f)
-            t_vq(f + 2)
-        for f in (l0 + 2, l0 + 3):
-            t_so(f - 2, 0)
-            t_so(f - 2, 1)
+            t_vq(f + 1)
+            if late < NB:
+                t_sqsum(late)
+            t_clamp(r, (2, 3))
+            for t in range(NT):
+                t_so(f, t)
+            if f == GB - 1:
+                t_const(5)
+
+        t_te(last[1], "P")
+        t_mx(last[0], (0, 1, 2, 3))
+        for i in range(1, n):
+            if i + 1 < n:
+                t_te(last[i + 1], "P" if i % 2 == 0 else "eT")
+            t_mx(last[i], (0, 1, 2, 3))
+
+        t_vq(last[1])
+        for i, f in enumerate(last):
+            if i >= 2:
+                t_so(last[i - 2], 0)
+                t_so(last[i - 2], 1)
             t_ce(f, 0)
+            if i < n - 2:
+                t_ce(f, 1)
             t_recip(f)
             t_qe(f)
-        for f in (l0 + 2, l0 + 3):
+            if i + 2 < n:
+                t_vq(last[i + 2])
+        for f in last[n - 2 :]:
             t_so(f, 0)
             t_so(f, 1)
-        for f in (l0, l0 + 1):
+
+        def act_so(f):
             t_so(f, 2, "act")
             t_so(f, 3, "act")
-            t_ce(f + 2, 1, "act")
-        for f in (l0 + 2, l0 + 3):
-            t_so(f, 2, "act")
-            t_so(f, 3, "act")
+
+        if n >= 4:
+            act_so(last[n - 4])
+        t_ce(last[n - 2], 1, "act")
+        if n >= 3:
+            act_so(last[n - 3])
+        t_ce(last[n - 1], 1, "act")
+        act_so(last[n - 2])
+        act_so(last[n - 1])
 
         done = set()
         at = {e: 0 for e in order}

@@ -28,6 +28,8 @@ GMAX = 5
 NX = 4
 NVG = 4
 AHEAD = 7
+SQUARES_AFTER_ROOTS = {0: (2, 3), 1: (4, 5), 2: (6, 7), 4: (12,), 5: (13,), 6: (14,), 7: (15,)}
+SQUARES_AFTER_LOGS = {0: (8,), 1: (9,), 2: (10,), 3: (11,)}
 CHUNKS = ((0,), (1,), (2, 3), (4, 5, 6, 7), (8, 9, 10, 11), (12, 13, 14, 15))
 NV = 3
 NVC = 4
@@ -412,11 +414,12 @@ def tile_hyperbolicattention_t_kernel(tc, query, keys, values, c, out):
         for group in GROUPS:
             for b in group:
                 t_roots(b)
-                if b == 0:
-                    t_sq(2)
-                    t_sq(3)
+                for s in SQUARES_AFTER_ROOTS.get(b, ()):
+                    t_sq(s)
             for b in group:
                 t_logs(b)
+                for s in SQUARES_AFTER_LOGS.get(b, ()):
+                    t_sq(s)
             for b in group:
                 t_exps(b)
 
@@ -436,19 +439,16 @@ def tile_hyperbolicattention_t_kernel(tc, query, keys, values, c, out):
             t_cross(b, (0, 1, 2, 3), "O")
             if b + 2 < GB:
                 t_tqk(b + 2)
-            t_clamp(b, squares_of=GB + b - 1 if b else None)
+            t_clamp(b)
             if b + 1 < 3:
                 t_const(b + 1)
             if b + 2 < GB:
                 t_cqk(b + 2)
-        for k in range(4):
-            t_sqpiece(2 * GB - 1, k)
         t_const(3)
         for b in range(GB, 2 * GB):
             t_tqk(b)
             t_cqk(b)
         for k in range(GB):
-            t_sqmul(2 * GB + k)
             for b in range(2 * GB + 2 * k, 2 * GB + 2 * k + 2):
                 t_tqk(b)
                 t_cqk(b)
@@ -456,7 +456,6 @@ def tile_hyperbolicattention_t_kernel(tc, query, keys, values, c, out):
                 t_cross(GB + k, (0, 1, 2, 3), "O")
             else:
                 t_cross(GB + k, (0, 1))
-            t_sqsum(2 * GB + k)
             if k < GB - 1:
                 t_clamp(GB + k)
         t_const(4)
@@ -468,7 +467,6 @@ def tile_hyperbolicattention_t_kernel(tc, query, keys, values, c, out):
         n = len(last)
         for f in range(last[0]):
             r = f + AHEAD
-            late = 3 * GB + f if f < GB else NB
             if f not in ends:
                 t_te(f + 1)
             t_cross(r, (2, 3))
@@ -480,12 +478,8 @@ def tile_hyperbolicattention_t_kernel(tc, query, keys, values, c, out):
             t_ce(f, 1)
             t_clamp(r, (0, 1))
             t_recip(f)
-            if late < NB:
-                t_sqmul(late)
             t_qe(f)
             t_vq(f + 1)
-            if late < NB:
-                t_sqsum(late)
             t_clamp(r, (2, 3))
             for t in range(NT):
                 t_so(f, t)

@@ -28,8 +28,7 @@ GMAX = 5
 NX = 4
 NVG = 4
 AHEAD = 7
-SQUARES_AFTER_ROOTS = {0: (2, 3), 1: (4, 5), 2: (6, 7), 4: (12,), 5: (13,), 6: (14,), 7: (15,)}
-SQUARES_AFTER_LOGS = {0: (8,), 1: (9,), 2: (10,), 3: (11,)}
+SQUARES_AFTER_ROOTS = {1: (4, 5), 2: (6, 7), 4: (12,), 5: (13,), 6: (14,), 7: (15,)}
 CHUNKS = ((0,), (1,), (2, 3), (4, 5, 6, 7), (8, 9, 10, 11), (12, 13, 14, 15))
 NV = 3
 NVC = 4
@@ -409,8 +408,8 @@ def tile_hyperbolicattention_t_kernel(tc, query, keys, values, c, out):
             t_st_half(f, 1, False)
             t_st_half(f, 0, True)
 
-        t_sq(0)
-        t_sq(1)
+        for b in range(GB):
+            t_sq(b)
         for group in GROUPS:
             for b in group:
                 t_roots(b)
@@ -418,8 +417,6 @@ def tile_hyperbolicattention_t_kernel(tc, query, keys, values, c, out):
                     t_sq(s)
             for b in group:
                 t_logs(b)
-                for s in SQUARES_AFTER_LOGS.get(b, ()):
-                    t_sq(s)
             for b in group:
                 t_exps(b)
 
@@ -449,6 +446,7 @@ def tile_hyperbolicattention_t_kernel(tc, query, keys, values, c, out):
             t_tqk(b)
             t_cqk(b)
         for k in range(GB):
+            t_sqmul(2 * GB + k)
             for b in range(2 * GB + 2 * k, 2 * GB + 2 * k + 2):
                 t_tqk(b)
                 t_cqk(b)
@@ -456,6 +454,7 @@ def tile_hyperbolicattention_t_kernel(tc, query, keys, values, c, out):
                 t_cross(GB + k, (0, 1, 2, 3), "O")
             else:
                 t_cross(GB + k, (0, 1))
+            t_sqsum(2 * GB + k)
             if k < GB - 1:
                 t_clamp(GB + k)
         t_const(4)

from contextlib import ExitStack
import math

import concourse.mybir as mybir
from concourse.masks import make_identity

F32 = mybir.dt.float32
BF16 = mybir.dt.bfloat16
U32 = mybir.dt.uint32
U8 = mybir.dt.uint8
FP8X4 = mybir.dt.float8_e4m3fn_x4
AF = mybir.ActivationFunctionType
ALU = mybir.AluOpType

NB, S, D, DV = 16, 512, 128, 512
P = 128
NT = S // P
EPS = 1e-6
KAPPA = 2.0 ** -21
INV_SCALE2 = 2.0 / math.sqrt(D)
W1 = S + 1
WP = S + 8
FLOPS = 2 * NB * S * S * (D + DV)

GB = 4
GROUPS = ((0, 1, 2, 3), (4, 5, 6, 7, 8), (9, 10, 11, 12, 13), (14, 15))
GMAX = 5
NX = 4
NVG = 4
AHEAD = 7
SQUARES_AFTER_ROOTS = {1: (4, 5), 2: (6, 7), 4: (12,), 5: (13,), 6: (14,), 7: (15,)}
CHUNKS = ((0,), (1,), (2, 3), (4, 5, 6, 7), (8, 9, 10, 11), (12, 13, 14, 15))
NV = 3
NVC = 4
NP_, NE_, NO_ = 2, 2, 4
G2N, B0, B1, HI, NK2H = 4, 5, 6, 7, 8


def tile_hyperbolicattention_t_kernel(tc, query, keys, values, c, out):
    nc = tc.nc
    with ExitStack() as ctx:
        ctx.enter_context(tc.manual_schedule())
        const = ctx.enter_context(tc.tile_pool(name="const", bufs=1))
        sqfp = ctx.enter_context(tc.tile_pool(name="sqfp", bufs=1))
        xp = ctx.enter_context(tc.tile_pool(name="xp", bufs=NX))
        rp = ctx.enter_context(tc.tile_pool(name="rp", bufs=GMAX))
        smallp = ctx.enter_context(tc.tile_pool(name="smallp", bufs=2 * GMAX))
        ep = ctx.enter_context(tc.tile_pool(name="ep", bufs=GMAX))
        grpp = ctx.enter_context(tc.tile_pool(name="grpp", bufs=2))
        ecp = ctx.enter_context(tc.tile_pool(name="ecp", bufs=2))
        vnp = ctx.enter_context(tc.tile_pool(name="vnp", bufs=NV))
        vgp = ctx.enter_context(tc.tile_pool(name="vgp", bufs=NVG))
        vcp = ctx.enter_context(tc.tile_pool(name="vcp", bufs=NVC))
        ostp = ctx.enter_context(tc.tile_pool(name="ostp", bufs=2))
        ps_p = ctx.enter_context(tc.psum_pool(name="ps_p", bufs=NP_))
        ps_e = ctx.enter_context(tc.psum_pool(name="ps_e", bufs=NE_))
        ps_o = ctx.enter_context(tc.psum_pool(name="ps_o", bufs=NO_))

        psum_of = {"P": ps_p, "eT": ps_e, "O": ps_o}
        chunk_of = {}
        for ci, ch in enumerate(CHUNKS):
            for b in ch:
                chunk_of[b] = ci

        def col(b, t):
            return (b - CHUNKS[chunk_of[b]][0]) * NT + t

        c_bf = const.tile([P, 1], BF16, name="c_bf")
        nc.sync.dma_start(out=c_bf[:], in_=c.partition_broadcast(P))
        ident_bf = const.tile([P, P], BF16, name="ident_bf")
        make_identity(nc, ident_bf[:])
        ident_f = const.tile([P, P], F32, name="ident_f")
        make_identity(nc, ident_f[:])
        one = const.tile([P, 1], F32, name="one")
        nc.vector.memset(one[:], 1.0)
        warm = const.tile([P, 1], F32, name="warm")
        nc.scalar.activation(out=warm[:], in_=one[:], func=AF.Sqrt)
        junk = const.tile([P, 2 * NT, D], BF16, name="junk")
        cc = const.tile([P, 8], F32, name="cc")
        cf, negc, neg2c, rc, e4c = (cc[:, i : i + 1] for i in range(5))
        nc.vector.tensor_copy(out=cf, in_=c_bf[:])
        nc.vector.tensor_scalar_mul(out=negc, in0=cf, scalar1=-1.0)
        nc.vector.tensor_scalar_mul(out=neg2c, in0=cf, scalar1=-2.0)
        nc.vector.reciprocal(out=rc, in_=cf)
        nc.vector.tensor_scalar_mul(out=e4c, in0=rc, scalar1=EPS / 4.0)

        qk, sq, cs, vn, SQF = {}, {}, {}, {}, {}
        qkps, qkT, X, R, EB, RS, RI, E, ET, GRP, EC, ES, VG, VC, VS, PS, O, OST = ({} for i in range(18))

        def load_qk(ci):
            ch = CHUNKS[ci]
            rows = slice(ch[0], ch[-1] + 1)
            qk[ci] = const.tile([P, len(ch), 2, S], BF16, name="qk%d" % ci)
            nc.sync.dma_start(out=qk[ci][:, :, 0, :], in_=query[rows].rearrange("b (p t) d -> p b (t d)", t=NT))
            nc.sync.dma_start(out=qk[ci][:, :, 1, :], in_=keys[rows].rearrange("b (p t) d -> p b (t d)", t=NT))
            sq[ci] = const.tile([P, 2, NT * len(ch)], F32, name="sq%d" % ci)

        def rows_of(w, b, t):
            ci = chunk_of[b]
            return qk[ci][:, b - CHUNKS[ci][0], w, t * D : (t + 1) * D]

        def load_values(b):
            vn[b] = vnp.tile([P, NT, DV], BF16, name="vn")
            nc.sync.dma_start(out=vn[b][:], in_=values[b].rearrange("(p t) v -> p t v", t=NT))

        def squares(b):
            for w in (1, 0):
                for t in range(NT):
                    nc.scalar.activation(
                        out=junk[:, w * NT + t, :], in_=rows_of(w, b, t), func=AF.Square,
                        accum_out=sq[chunk_of[b]][:, w, col(b, t) : col(b, t) + 1],
                    )

        def square_mul(b):
            ci = chunk_of[b]
            SQF[b] = sqfp.tile([P, 2 * S], F32, name="sqf")
            src = qk[ci][:, b - CHUNKS[ci][0], :, :].rearrange("p w s -> p (w s)")
            nc.vector.tensor_tensor(out=SQF[b][:], in0=src, in1=src, op=ALU.mult)

        def square_sum(b):
            nc.vector.tensor_reduce(
                out=sq[chunk_of[b]][:, :, col(b, 0) : col(b, 0) + NT],
                in_=SQF[b][:].rearrange("p (w t d) -> p w t d", w=2, t=NT),
                axis=mybir.AxisListType.X, op=ALU.add,
            )

        def square_piece(b, k):
            ci = chunk_of[b]
            w = k % 2
            if k == 0:
                SQF[b] = sqfp.tile([P, 2 * S], F32, name="sqf")
            half = SQF[b][:, w * S : (w + 1) * S]
            if k < 2:
                src = qk[ci][:, b - CHUNKS[ci][0], w, :]
                nc.vector.tensor_tensor(out=half, in0=src, in1=src, op=ALU.mult)
            else:
                nc.vector.tensor_reduce(
                    out=sq[ci][:, w, col(b, 0) : col(b, 0) + NT], in_=half.rearrange("p (t d) -> p t d", t=NT),
                    axis=mybir.AxisListType.X, op=ALU.add,
                )

        def constants(ci):
            n = NT * len(CHUNKS[ci])
            t_ = const.tile([P, 9, n], F32, name="cs%d" % ci)
            cs[ci] = t_
            q2, k2 = sq[ci][:, 0, :], sq[ci][:, 1, :]
            nc.vector.tensor_scalar_mul(out=t_[:, NK2H, :], in0=k2, scalar1=-0.5)
            nc.vector.tensor_scalar(out=t_[:, 0:2, :], in0=sq[ci][:], scalar1=negc, scalar2=1.0, op0=ALU.mult, op1=ALU.add)
            den = t_[:, 2, :]
            nc.vector.tensor_tensor(out=den, in0=t_[:, 0, :], in1=t_[:, 1, :], op=ALU.mult)
            nc.vector.tensor_scalar_max(out=den, in0=den, scalar1=EPS)
            nc.vector.tensor_scalar(out=t_[:, 0, :], in0=den, scalar1=e4c, scalar2=None, op0=ALU.mult)
            nc.vector.reciprocal(out=t_[:, 3, :], in_=den)
            nc.vector.scalar_tensor_tensor(out=t_[:, HI, :], in0=q2, scalar=(1.0 - KAPPA) / 2.0, in1=t_[:, 0, :], op0=ALU.mult, op1=ALU.subtract)
            nc.vector.tensor_scalar(out=t_[:, G2N, :], in0=t_[:, 3, :], scalar1=neg2c, scalar2=None, op0=ALU.mult)
            nc.vector.scalar_tensor_tensor(out=t_[:, B0, :], in0=t_[:, 3, :], scalar=cf, in1=q2, op0=ALU.mult, op1=ALU.mult)
            nc.vector.tensor_scalar_add(out=t_[:, B1, :], in0=t_[:, B0, :], scalar1=1.0)

        def cst(b, t, row):
            return cs[chunk_of[b]][:, row, col(b, t) : col(b, t) + 1]

        def transpose_qk(b):
            qkps[b] = ps_o.tile([P, 2 * S], BF16, name="O")
            for w in range(2):
                for t in range(NT):
                    nc.tensor.transpose(qkps[b][:, w * S + t * P : w * S + (t + 1) * P], rows_of(w, b, t), ident_bf[:])

        def copy_qk(b):
            qkT[b] = const.tile([P, 2 * S], BF16, name="qkT%d" % b)
            nc.vector.tensor_copy(out=qkT[b][:], in_=qkps[b][:])

        def cross(b, t, ring_name):
            ps = psum_of[ring_name].tile([P, S], F32, name=ring_name)
            PS[b, t] = ps
            nc.tensor.matmul(out=ps[:], lhsT=qkT[b][:, t * P : (t + 1) * P], rhs=qkT[b][:, S : 2 * S], start=True, stop=False)
            for tj in range(NT):
                nc.tensor.matmul(
                    out=ps[:, tj * P : (tj + 1) * P], lhsT=cst(b, tj, NK2H).to_broadcast([P, P]), rhs=ident_f[:],
                    is_transpose=True, start=False, stop=(tj == NT - 1),
                )

        def clamp(b, t):
            if t == 0:
                X[b] = xp.tile([P, NT, WP], F32, name="X")
            nc.vector.tensor_scalar(
                out=X[b][:, t, 0:S], in0=PS[b, t][:], scalar1=cst(b, t, HI), scalar2=None,
                op0=ALU.min, op1=ALU.max, accum_out=X[b][:, t, S:W1],
            )

        def roots(b):
            R[b] = rp.tile([P, NT, WP], F32, name="R")
            for t in range(NT + 1):
                if t < NT:
                    nc.scalar.activation(out=R[b][:, t, 0:W1], in_=X[b][:, t, 0:W1], func=AF.Sqrt, bias=cst(b, t, B1), scale=cst(b, t, G2N))
                if t > 0:
                    u = t - 1
                    nc.scalar.activation(out=X[b][:, u, 0:W1], in_=X[b][:, u, 0:W1], func=AF.Sqrt, bias=cst(b, u, B0), scale=cst(b, u, G2N))

        def add_roots(b):
            for t in range(NT):
                nc.gpsimd.tensor_tensor(out=R[b][:, t, 0:W1], in0=R[b][:, t, 0:W1], in1=X[b][:, t, 0:W1], op=ALU.add)

        def logs(b):
            nc.scalar.activation(out=R[b][:, :, 0:W1], in_=R[b][:, :, 0:W1], func=AF.Ln)

        def exp_bias(b):
            EB[b] = smallp.tile([P, NT], F32, name="eb")
            nc.gpsimd.tensor_scalar(
                out=EB[b][:].unsqueeze(2), in0=R[b][:, :, S:W1], scalar1=INV_SCALE2, scalar2=0.0, op0=ALU.mult, op1=ALU.add,
            )

        def exps(b):
            E[b] = ep.tile([P, NT, S], BF16, name="e")
            RS[b] = smallp.tile([P, NT], F32, name="rs")
            for t in range(NT):
                nc.scalar.activation(
                    out=E[b][:, t, :], in_=R[b][:, t, 0:S], func=AF.Exp,
                    bias=EB[b][:, t : t + 1], scale=-INV_SCALE2, accum_out=RS[b][:, t : t + 1],
                )

        def recip(b):
            RI[b] = smallp.tile([P, NT], F32, name="ri")
            nc.vector.reciprocal(out=RI[b][:], in_=RS[b][:])

        def transpose_e(b, h, ring_name):
            ET[b, h] = psum_of[ring_name].tile([P, 2, NT, P], BF16, name=ring_name)
            for a in range(2):
                for tj in range(NT):
                    nc.tensor.transpose(ET[b, h][:, a, tj, :], E[b][:, 2 * h + a, tj * P : (tj + 1) * P], ident_bf[:])

        def copy_e(b, h, eng):
            if h == 0:
                GRP[b] = grpp.tile([P, S, NT], BF16, name="grp", align_bytes=64)
            dst = GRP[b][:, h * 2 * P : (h + 1) * 2 * P, :].rearrange("p (a i) t -> p a i t", a=2)
            src = ET[b, h][:].rearrange("p a t i -> p a i t")
            if eng == "act":
                nc.scalar.copy(out=dst, in_=src)
            else:
                nc.vector.tensor_copy(out=dst, in_=src)

        def quantise_e(b):
            EC[b] = ecp.tile([P, S], U32, name="ec", align_bytes=64)
            ES[b] = ecp.tile([P, S], U8, name="es", align_bytes=64)
            nc.vector.quantize_mx(out=EC[b][:].bitcast(FP8X4), scales=ES[b][:], in_=GRP[b][:].rearrange("p i t -> p (i t)"))

        def regroup_v(b):
            VG[b] = vgp.tile([P, DV, NT], BF16, name="vg", align_bytes=64)
            for k in range(NT):
                cols = slice(k * P, (k + 1) * P)
                nc.gpsimd.tensor_scalar(
                    out=VG[b][:, cols, :], in0=vn[b][:, :, cols].rearrange("p t v -> p v t"),
                    scalar1=1.0, scalar2=0.0, op0=ALU.mult, op1=ALU.add,
                )

        def quantise_v(b):
            VC[b] = vcp.tile([P, DV], U32, name="vc", align_bytes=64)
            VS[b] = vcp.tile([P, DV], U8, name="vs", align_bytes=64)
            nc.vector.quantize_mx(out=VC[b][:].bitcast(FP8X4), scales=VS[b][:], in_=VG[b][:].rearrange("p v t -> p (v t)"))

        def mx(b, t, ring_name):
            O[b, t] = psum_of[ring_name].tile([P, DV], F32, name=ring_name)
            cols = slice(t * P, (t + 1) * P)
            nc.tensor.matmul_mx(
                out=O[b, t][:], lhsT=EC[b][:, cols].bitcast(FP8X4), lhsT_scale=ES[b][:, cols],
                rhs=VC[b][:].bitcast(FP8X4), rhs_scale=VS[b][:], start=True, stop=True,
            )

        def scale_out(b, t, eng):
            if b not in OST:
                OST[b] = ostp.tile([P, NT, DV], F32, name="ost")
            if eng == "act":
                nc.scalar.activation(out=OST[b][:, t, :], in_=O[b, t][:], func=AF.Copy, scale=RI[b][:, t : t + 1])
            else:
                nc.vector.tensor_scalar_mul(out=OST[b][:, t, :], in0=O[b, t][:], scalar1=RI[b][:, t : t + 1])

        def store(b, tiles):
            nc.sync.dma_start(out=out[b].rearrange("(p t) v -> p t v", t=NT)[:, tiles, :], in_=OST[b][:, tiles, :])

        order = {"act": [], "dve": [], "pe": [], "pool": [], "sp": []}
        ring = {"P": [], "eT": [], "O": []}
        depth_of = {"P": NP_, "eT": NE_, "O": NO_}

        def add(eng, key, needs, fn):
            order[eng].append((key, [n for n in needs if n is not None], fn))

        def back(name, key, depth):
            lst = ring[name]
            lst.append(key)
            return lst[-1 - depth] if len(lst) > depth else None

        def ok(kind, b, *rest):
            return (kind, b) + rest if 0 <= b < NB else None

        def t_sq(b):
            add("act", ("sq", b), [("ldqk", chunk_of[b])], lambda: squares(b))

        def t_sqmul(b):
            add("dve", ("sqmul", b), [("ldqk", chunk_of[b]), ok("sq", b - 1)], lambda: square_mul(b))

        def t_sqsum(b):
            add("dve", ("sq", b), [("sqmul", b)], lambda: square_sum(b))

        def t_sqpiece(b, k):
            key = ("sq", b) if k == 3 else ("sqpiece", b, k)
            before = ("sqpiece", b, k - 1) if k else (("sq", b - 1) if b > GB else None)
            add("dve", key, [("ldqk", chunk_of[b]), before], lambda: square_piece(b, k))

        def t_roots(b):
            add("act", ("roots", b), [("clamp", b, t) for t in range(NT)] + [ok("exps", b - GMAX)], lambda: roots(b))

        def t_logs(b):
            add("act", ("logs", b), [("add", b)], lambda: logs(b))

        def t_exps(b):
            add("act", ("exps", b), [("eb", b), ok("te", b - GMAX, 1)], lambda: exps(b))

        def t_eb(b):
            add("pool", ("eb", b), [("logs", b)], lambda: exp_bias(b))

        def t_const(ci):
            add("dve", ("const", ci), [("sq", b) for b in CHUNKS[ci]], lambda: constants(ci))

        def t_tqk(b):
            add("pe", ("tqk", b), [("ldqk", chunk_of[b]), back("O", ("cqk", b), NO_)], lambda: transpose_qk(b))

        def t_cqk(b):
            add("dve", ("cqk", b), [("tqk", b)], lambda: copy_qk(b))

        def t_cross(b, tiles, ring_name="P"):
            if b < NB:
                for t in tiles:
                    freed = back(ring_name, ("clamp", b, t), depth_of[ring_name])
                    add("pe", ("cross", b, t), [("cqk", b), ("const", chunk_of[b]), freed], lambda t=t: cross(b, t, ring_name))

        def t_clamp(b, tiles=(0, 1, 2, 3), squares_of=None):
            if b < NB:
                for t in tiles:
                    add("dve", ("clamp", b, t), [("cross", b, t), ok("add", b - NX)], lambda t=t: clamp(b, t))
                    if squares_of is not None:
                        t_sqpiece(squares_of, t)

        def t_add(b):
            add("pool", ("add", b), [("roots", b)], lambda: add_roots(b))

        def t_te(b, ring_name="eT"):
            if b < NB:
                for h in range(2):
                    freed = back(ring_name, ("ce", b, h), depth_of[ring_name])
                    add("pe", ("te", b, h), [("exps", b), freed], lambda h=h: transpose_e(b, h, ring_name))

        def t_ce(b, h, eng="dve"):
            add(eng, ("ce", b, h), [("te", b, h), ok("qe", b - 2), ("ce", b, 0) if h else None], lambda: copy_e(b, h, eng))

        def t_qe(b):
            add("dve", ("qe", b), [("ce", b, 0), ("ce", b, 1), ok("mx", b - 2, NT - 1)], lambda: quantise_e(b))

        def t_vr(b):
            add("pool", ("vr", b), [("ldv", b), ok("vq", b - NVG)], lambda: regroup_v(b))

        def t_vq(b):
            if b < NB:
                add("dve", ("vq", b), [("vr", b), ok("mx", b - NVC, NT - 1)], lambda: quantise_v(b))

        def t_mx(b, tiles, ring_name="O"):
            for t in tiles:
                freed = back(ring_name, ("so", b, t), depth_of[ring_name])
                add("pe", ("mx", b, t), [("qe", b), ("vq", b), freed], lambda t=t: mx(b, t, ring_name))

        def t_recip(b):
            add("dve", ("recip", b), [("exps", b)], lambda: recip(b))

        def t_so(b, t, eng="dve"):
            add(eng, ("so", b, t), [("mx", b, t), ("recip", b), ok("st", b - 2)], lambda: scale_out(b, t, eng))

        def t_st(b):
            add("sp", ("st", b), [("so", b, t) for t in range(NT)], lambda: store(b, slice(0, NT)))

        def t_st_half(b, h, last):
            key = ("st", b) if last else ("st_first", b)
            add("sp", key, [("so", b, 2 * h), ("so", b, 2 * h + 1)], lambda: store(b, slice(2 * h, 2 * h + 2)))

        def t_ldv(b):
            if b < NB:
                add("sp", ("ldv", b), [ok("vr", b - NV)], lambda: load_values(b))

        def t_ldqk(ci):
            add("sp", ("ldqk", ci), [], lambda: load_qk(ci))

        for ci in (0, 1, 2, 3):
            t_ldqk(ci)
        t_ldv(0)
        t_ldqk(4)
        t_ldqk(5)
        t_ldv(1)
        t_ldv(2)
        for b in range(GB):
            t_ldv(b + NV)
        for gi in range(1, len(GROUPS)):
            loads = [b + NV for b in GROUPS[gi]]
            for k, f in enumerate(GROUPS[gi - 1]):
                t_st(f)
                if k >= 1:
                    for b in loads[2 * k - 2 : 2 * k]:
                        t_ldv(b)
            for b in loads[2 * len(GROUPS[gi - 1]) - 2 :]:
                t_ldv(b)
        for f in GROUPS[-1]:
            t_st_half(f, 1, False)
            t_st_half(f, 0, True)

        for b in range(GB):
            t_sq(b)
        for group in GROUPS:
            for b in group:
                t_roots(b)
                for s in SQUARES_AFTER_ROOTS.get(b, ()):
                    t_sq(s)
            for b in group:
                t_logs(b)
            for b in group:
                t_exps(b)

        for group in GROUPS:
            for b in group:
                t_add(b)
            for b in group:
                t_vr(b)
                t_eb(b)

        t_tqk(0)
        t_tqk(1)
        t_cqk(0)
        t_const(0)
        t_cqk(1)
        for b in range(GB):
            t_cross(b, (0, 1, 2, 3), "O")
            if b + 2 < GB:
                t_tqk(b + 2)
            t_clamp(b)
            if b + 1 < 3:
                t_const(b + 1)
            if b + 2 < GB:
                t_cqk(b + 2)
        t_const(3)
        for b in range(GB, 2 * GB):
            t_tqk(b)
            t_cqk(b)
        for k in range(GB):
            t_sqmul(2 * GB + k)
            for b in range(2 * GB + 2 * k, 2 * GB + 2 * k + 2):
                t_tqk(b)
                t_cqk(b)
            if k < GB - 1:
                t_cross(GB + k, (0, 1, 2, 3), "O")
            else:
                t_cross(GB + k, (0, 1))
            t_sqsum(2 * GB + k)
            if k < GB - 1:
                t_clamp(GB + k)
        t_const(4)
        t_vq(0)
        t_te(0)

        ends = [group[-1] for group in GROUPS]
        last = GROUPS[-1]
        n = len(last)
        for f in range(last[0]):
            r = f + AHEAD
            if f not in ends:
                t_te(f + 1)
            t_cross(r, (2, 3))
            t_mx(f, (0, 1, 2, 3))
            t_cross(r + 1, (0, 1))
            if f in ends:
                t_te(f + 1)
            t_ce(f, 0)
            t_ce(f, 1)
            t_clamp(r, (0, 1))
            t_recip(f)
            t_qe(f)
            t_vq(f + 1)
            t_clamp(r, (2, 3))
            for t in range(NT):
                t_so(f, t)
            if f == GB - 1:
                t_const(5)

        t_te(last[1], "P")
        t_mx(last[0], (0, 1, 2, 3))
        for i in range(1, n):
            if i + 1 < n:
                t_te(last[i + 1], "P" if i % 2 == 0 else "eT")
            t_mx(last[i], (0, 1, 2, 3))

        t_vq(last[1])
        for i, f in enumerate(last):
            if i >= 2:
                t_so(last[i - 2], 0)
                t_so(last[i - 2], 1)
            t_ce(f, 0)
            if i < n - 2:
                t_ce(f, 1)
            t_recip(f)
            t_qe(f)
            if i + 2 < n:
                t_vq(last[i + 2])
        for f in last[n - 2 :]:
            t_so(f, 0)
            t_so(f, 1)

        def act_so(f):
            t_so(f, 2, "act")
            t_so(f, 3, "act")

        if n >= 4:
            act_so(last[n - 4])
        t_ce(last[n - 2], 1, "act")
        if n >= 3:
            act_so(last[n - 3])
        t_ce(last[n - 1], 1, "act")
        act_so(last[n - 2])
        act_so(last[n - 1])

        done = set()
        at = {e: 0 for e in order}
        left = sum(len(v) for v in order.values())
        while left:
            moved = 0
            for e in ("sp", "act", "pe", "pool", "dve"):
                while at[e] < len(order[e]) and all(n in done for n in order[e][at[e]][1]):
                    key, needs, fn = order[e][at[e]]
                    fn()
                    done.add(key)
                    at[e] += 1
                    moved += 1
            assert moved, "the orders of the engines contradict each other"
            left -= moved
